import numpy as np
import ml_dtypes


def mxq(x, axis, fmt="e4m3"):
    dtype, down = {"e4m3": (ml_dtypes.float8_e4m3fn, 7), "e5m2": (ml_dtypes.float8_e5m2, 14)}[fmt]
    v = np.moveaxis(np.asarray(x, np.float32).astype(ml_dtypes.bfloat16).astype(np.float64), axis, -1)
    blocks = v.reshape(v.shape[:-1] + (-1, 32))
    amax = np.abs(blocks).max(-1, keepdims=True)
    byte = np.maximum(np.where(amax > 0, np.frexp(amax)[1] - 1 + 127, 0) - down, 1)
    scale = np.exp2(byte - 127.0)
    codes = (blocks / scale).astype(np.float32).astype(dtype).astype(np.float64)
    return np.moveaxis((codes * scale).reshape(v.shape), -1, axis)


WIDE = False


def mx_kscale(k):
    if not WIDE:
        return np.ones(k)
    levels = np.array([10, -10, 5, -5, 0])
    a = np.random.permutation(np.resize(levels, k // 512 * 4)).reshape(k // 512, 4)
    idx = np.arange(k)
    return np.exp2(a[idx // 512, idx % 128 // 32])


BF16 = ml_dtypes.bfloat16


def bf(x):
    return np.asarray(x, np.float32).astype(BF16)


def f64(x):
    return np.asarray(x).astype(np.float64)


E2M1 = np.array([0.0, 0.5, 1.0, 1.5, 2.0, 3.0, 4.0, 6.0, -0.0, -0.5, -1.0, -1.5, -2.0, -3.0, -4.0, -6.0])


def pack_weight(w, fmt):
    k, n = w.shape
    w = f64(bf(w)).reshape(k // 32, 32, n)
    amax = np.abs(w).max(1)
    if fmt == "e4m3":
        byte = np.frexp(amax)[1] - 1 + 127 - 7
    else:
        mant, ex = np.frexp(amax / 6.0)
        byte = np.where(mant > 0.5, ex, ex - 1) + 127
    byte = np.clip(np.where(amax > 0, byte, 1), 1, 254)
    scaled = (w * np.exp2(127.0 - byte)[:, None, :]).reshape(k, n).astype(np.float32)
    by_word = np.ascontiguousarray(scaled.reshape(k // 512, 128, 4, n).transpose(0, 1, 3, 2))
    if fmt == "e4m3":
        words = by_word.astype(ml_dtypes.float8_e4m3fn).view(np.uint8)
    else:
        c = by_word.astype(ml_dtypes.float4_e2m1fn).view(np.uint8) & 0xF
        words = c[..., 0::2] | (c[..., 1::2] << 4)
    return np.ascontiguousarray(words), np.ascontiguousarray(byte.astype(np.uint8).reshape(k // 512, 16, n))


def unpack_weight(words, scales, fmt):
    g, p, n, _ = words.shape
    if fmt == "e4m3":
        vals = np.ascontiguousarray(words).view(ml_dtypes.float8_e4m3fn).astype(np.float64)
    else:
        nib = np.empty((g, p, n, 4), np.uint8)
        nib[..., 0::2] = words & 0xF
        nib[..., 1::2] = words >> 4
        vals = E2M1[nib]
    vals = vals * np.repeat(np.exp2(scales.astype(np.float64) - 127.0), 8, axis=1)[..., None]
    return vals.transpose(0, 1, 3, 2).reshape(g * 512, n)


N, F, H = 1024, 8192, 512
SIG = 1.5


def draw_adj():
    r = np.random.uniform(0.5, 1.5, (N, 1))
    return 2.0 * r * np.exp(SIG * np.random.standard_normal((N, N)) - 0.5 * SIG * SIG) / N


def setup_inputs():
    s, t = mx_kscale(F), mx_kscale(N)
    x_init = bf(np.random.standard_normal((N, F)) * s / t[:, None])
    adj1 = bf(draw_adj() * t)
    W1_words, W1_scales = pack_weight(np.random.standard_normal((F, H)) * 4.0 / np.sqrt(F) / s[:, None], "e4m3")
    b1 = bf(np.random.standard_normal(H) * 0.3)
    return {"x_init": x_init,
            "adj1": adj1,
            "W1_words": W1_words,
            "W1_scales": W1_scales,
            "b1": b1}


def reference(x_init, adj1, W1_words, W1_scales, b1):
    support = mxq(f64(x_init), 1, "e4m3") @ unpack_weight(W1_words, W1_scales, "e4m3")
    y = (mxq(f64(adj1), 1, "e4m3") @ mxq(support, 0, "e4m3")) + f64(b1)
    return np.maximum(y, 0.0)

@@ -1,0 +1,217 @@
+import concourse.mybir as mybir
+from concourse.masks import make_identity
+
+BF16 = mybir.dt.bfloat16
+F32 = mybir.dt.float32
+I32 = mybir.dt.int32
+U32 = mybir.dt.uint32
+U8 = mybir.dt.uint8
+FP8X4 = mybir.dt.float8_e4m3fn_x4
+
+P = 128
+PACK = 4
+K_PASS = P * PACK
+NODES, FEATURES, HIDDEN = 1024, 8192, 512
+
+HALVES = NODES // K_PASS
+CHUNK_PASSES = 4
+CHUNKS = FEATURES // (CHUNK_PASSES * K_PASS)
+CHUNK = CHUNK_PASSES * K_PASS
+SEGMENTS = 8
+BANK_SEGMENTS = 2
+BLOCK_TILES = SEGMENTS // CHUNK_PASSES
+ADJ_BLOCK_TILES = SEGMENTS // HALVES
+ROW_TILES = NODES // P
+LOADS_AHEAD = 4
+
+FLOPS = 2 * NODES * FEATURES * HIDDEN + 2 * NODES * NODES * HIDDEN
+
+
+def tile_gcn_pa_k_kernel(tc, x_init, adj1, W1_words, W1_scales, b1, out):
+    nc = tc.nc
+
+    blocks = []
+    for s in range(HALVES):
+        for c in range(CHUNKS):
+            for h in range(PACK // BLOCK_TILES):
+                blocks.append(("x", s, c, h))
+            if s == HALVES - 1 and c < ROW_TILES // ADJ_BLOCK_TILES:
+                blocks.append(("adj", c, 0, 0))
+
+    with tc.manual_schedule(), tc.tile_pool(name="resident", bufs=1) as resident, tc.tile_pool(
+        name="raw", bufs=LOADS_AHEAD + 1
+    ) as raw_pool, tc.tile_pool(name="stream", bufs=3) as stream, tc.tile_pool(
+        name="support", bufs=2
+    ) as support_pool, tc.tile_pool(name="rows", bufs=4) as rows_pool:
+        identity = resident.tile([P, P], F32)
+        make_identity(nc, identity[:])
+
+        w_codes = resident.tile([P, CHUNKS * CHUNK_PASSES, HIDDEN], U32, align_bytes=64)
+        w_scales = resident.tile([P, CHUNKS, HIDDEN], U8, align_bytes=64)
+        nc.vector.memset(w_scales[:].bitcast(I32), 0)
+
+        adj_codes = resident.tile([P, ROW_TILES * HALVES, P], U32, align_bytes=64)
+        adj_scales = resident.tile([P, ROW_TILES * HALVES, P], U8, align_bytes=64)
+        support_codes = resident.tile([P, HALVES, HIDDEN], U32, align_bytes=64)
+        support_scales = resident.tile([P, HALVES, HIDDEN], U8, align_bytes=64)
+        bias = resident.tile([P, HIDDEN], BF16)
+
+        raw_of = {}
+        sorted_of = {}
+        codes_of = {}
+        support_sum = {}
+        support_rows = {}
+
+        def load_weight_chunk(c):
+            passes = slice(c * CHUNK_PASSES, (c + 1) * CHUNK_PASSES)
+            for quadrant in range(4):
+                nc.sync.dma_start(
+                    out=w_scales[32 * quadrant : 32 * quadrant + 16, c, :].bitcast(I32),
+                    in_=W1_scales[passes, 4 * quadrant : 4 * quadrant + 4, :].bitcast(I32),
+                )
+            nc.sync.dma_start(
+                out=w_codes[:, passes, :].bitcast(I32),
+                in_=W1_words[passes].rearrange("g p n t -> p g (n t)").bitcast(I32),
+            )
+
+        def load(j):
+            kind, s, c, h = blocks[j]
+            raw = raw_pool.tile([P, SEGMENTS, K_PASS], BF16)
+            raw_of[j] = raw
+            if kind == "x":
+                tiles = slice(h * BLOCK_TILES, (h + 1) * BLOCK_TILES)
+                nc.sync.dma_start(
+                    out=raw[:].rearrange("p (t g) k -> p t (g k)", t=BLOCK_TILES),
+                    in_=x_init[s * K_PASS : (s + 1) * K_PASS, c * CHUNK : (c + 1) * CHUNK].rearrange(
+                        "(p t) f -> p t f", t=PACK
+                    )[:, tiles, :],
+                )
+                if s == 0 and h == PACK // BLOCK_TILES - 1:
+                    load_weight_chunk(c)
+            else:
+                nc.sync.dma_start(
+                    out=raw[:].rearrange("p s k -> p (s k)"),
+                    in_=adj1[s * K_PASS : (s + 1) * K_PASS, :].rearrange(
+                        "(p a) k -> p (a k)", a=ADJ_BLOCK_TILES
+                    ),
+                )
+
+        def sort_words(j):
+            words = stream.tile([P, SEGMENTS, 2, P], F32)
+            sorted_of[j] = words
+            nc.vector.tensor_copy(
+                out=words[:],
+                in_=raw_of[j][:].bitcast(F32).rearrange("r s (p u) -> r s u p", u=2),
+            )
+
+        def transpose_and_quantise(j):
+            kind, s, c, h = blocks[j]
+            grouped = stream.tile([P, SEGMENTS, P, PACK], BF16, align_bytes=64)
+            for bank in range(SEGMENTS // BANK_SEGMENTS):
+                first = bank * BANK_SEGMENTS
+                planes = transposed.tile([P, BANK_SEGMENTS, 2, P], F32)
+                for i in range(BANK_SEGMENTS):
+                    for u in range(2):
+                        nc.tensor.transpose(
+                            planes[:, i, u, :], sorted_of[j][:, first + i, u, :], identity[:]
+                        )
+                nc.scalar.copy(
+                    out=grouped[:, first : first + BANK_SEGMENTS, :, :].bitcast(F32),
+                    in_=planes[:].rearrange("p s u r -> p s r u"),
+                )
+            if kind == "x":
+                codes = stream.tile([P, SEGMENTS, P], U32, align_bytes=64)
+                scales = stream.tile([P, SEGMENTS, P], U8, align_bytes=64)
+                codes_of[j] = (codes[:], scales[:])
+            else:
+                segments = slice(s * SEGMENTS, (s + 1) * SEGMENTS)
+                codes_of[j] = (adj_codes[:, segments, :], adj_scales[:, segments, :])
+            nc.vector.quantize_mx(
+                out=codes_of[j][0].rearrange("p s r -> p (s r)").bitcast(FP8X4),
+                scales=codes_of[j][1].rearrange("p s r -> p (s r)"),
+                in_=grouped[:].rearrange("p s r t -> p (s r t)"),
+            )
+
+        def multiply(j):
+            kind, s, c, h = blocks[j]
+            if kind != "x":
+                return
+            codes, scales = codes_of[j]
+            for i in range(BLOCK_TILES):
+                t = h * BLOCK_TILES + i
+                if c == 0:
+                    sums = sums_pool.tile([P, HIDDEN], F32, name="support_sum%d" % t)
+                    support_sum[t] = sums
+                for g in range(CHUNK_PASSES):
+                    nc.tensor.matmul_mx(
+                        out=support_sum[t][:],
+                        lhsT=codes[:, i * CHUNK_PASSES + g, :].bitcast(FP8X4),
+                        lhsT_scale=scales[:, i * CHUNK_PASSES + g, :],
+                        rhs=w_codes[:, c * CHUNK_PASSES + g, :].bitcast(FP8X4),
+                        rhs_scale=w_scales[4 * g : P, c, :],
+                        start=(c == 0 and g == 0),
+                        stop=(c == CHUNKS - 1 and g == CHUNK_PASSES - 1),
+                    )
+            if c == CHUNKS - 1:
+                quantise_support(s, h)
+
+        def quantise_support(s, h):
+            if h == 0:
+                rounded = support_pool.tile([P, PACK, HIDDEN], BF16)
+                support_rows[s] = rounded
+            for t in range(h * BLOCK_TILES, (h + 1) * BLOCK_TILES):
+                nc.scalar.copy(out=support_rows[s][:, t, :], in_=support_sum[t][:])
+            if h == PACK // BLOCK_TILES - 1:
+                grouped = support_pool.tile([P, HIDDEN, PACK], BF16, align_bytes=64)
+                nc.vector.tensor_copy(
+                    out=grouped[:], in_=support_rows[s][:].rearrange("p t n -> p n t")
+                )
+                nc.vector.quantize_mx(
+                    out=support_codes[:, s, :].bitcast(FP8X4),
+                    scales=support_scales[:, s, :],
+                    in_=grouped[:].rearrange("p n t -> p (n t)"),
+                )
+
+        with tc.psum_pool(name="transposed", bufs=4) as transposed, tc.psum_pool(
+            name="sums", bufs=1
+        ) as sums_pool:
+            for step in range(len(blocks) + LOADS_AHEAD + 2):
+                if step < len(blocks):
+                    load(step)
+                if 0 <= step - LOADS_AHEAD < len(blocks):
+                    sort_words(step - LOADS_AHEAD)
+                if 0 <= step - LOADS_AHEAD - 1 < len(blocks):
+                    transpose_and_quantise(step - LOADS_AHEAD - 1)
+                if 0 <= step - LOADS_AHEAD - 2 < len(blocks):
+                    multiply(step - LOADS_AHEAD - 2)
+
+        nc.sync.dma_start(out=bias[:], in_=b1.partition_broadcast(P))
+
+        out_tiles = out.rearrange("(b r i) n -> b i r n", r=P, i=ADJ_BLOCK_TILES)
+        with tc.psum_pool(name="y", bufs=ROW_TILES, reuse_waits="tile") as y_pool:
+            y_sums = []
+            for a in range(ROW_TILES):
+                y_sum = y_pool.tile([P, HIDDEN], F32)
+                y_sums.append(y_sum)
+            for s in range(HALVES):
+                for a in range(ROW_TILES):
+                    nc.tensor.matmul_mx(
+                        out=y_sums[a][:],
+                        lhsT=adj_codes[:, a * HALVES + s, :].bitcast(FP8X4),
+                        lhsT_scale=adj_scales[:, a * HALVES + s, :],
+                        rhs=support_codes[:, s, :].bitcast(FP8X4),
+                        rhs_scale=support_scales[:, s, :],
+                        start=(s == 0),
+                        stop=(s == HALVES - 1),
+                    )
+            for a in range(ROW_TILES):
+                y_rows = rows_pool.tile([P, HIDDEN], F32)
+                nc.vector.tensor_tensor(
+                    out=y_rows[:], in0=y_sums[a][:], in1=bias[:], op=mybir.AluOpType.add
+                )
+                nc.scalar.activation(
+                    out=y_rows[:], in_=y_rows[:], func=mybir.ActivationFunctionType.Relu
+                )
+                nc.sync.dma_start(
+                    out=out_tiles[a // ADJ_BLOCK_TILES, a % ADJ_BLOCK_TILES], in_=y_rows[:]
+                )

@@ -14,15 +14,15 @@ K_PASS = P * PACK
 NODES, FEATURES, HIDDEN = 1024, 8192, 512
 
 HALVES = NODES // K_PASS
-CHUNK_PASSES = 4
-CHUNKS = FEATURES // (CHUNK_PASSES * K_PASS)
-CHUNK = CHUNK_PASSES * K_PASS
-SEGMENTS = 8
+PIECE_SEGMENTS = 4
+PIECE = PIECE_SEGMENTS * K_PASS
+CHUNKS = FEATURES // PIECE
 BANK_SEGMENTS = 2
-BLOCK_TILES = SEGMENTS // CHUNK_PASSES
-ADJ_BLOCK_TILES = SEGMENTS // HALVES
+BLOCK_TILES = 2
+HALF_BLOCKS = PACK // BLOCK_TILES
 ROW_TILES = NODES // P
-LOADS_AHEAD = 4
+PIECE_ROW_TILES = PIECE // NODES
+LOADS_AHEAD = 3
 
 FLOPS = 2 * NODES * FEATURES * HIDDEN + 2 * NODES * NODES * HIDDEN
 
@@ -33,20 +33,27 @@ def tile_gcn_pa_k_kernel(tc, x_init, adj1, W1_words, W1_scales, b1, out):
     blocks = []
     for s in range(HALVES):
         for c in range(CHUNKS):
-            for h in range(PACK // BLOCK_TILES):
-                blocks.append(("x", s, c, h))
-            if s == HALVES - 1 and c < ROW_TILES // ADJ_BLOCK_TILES:
-                blocks.append(("adj", c, 0, 0))
+            for h in range(HALF_BLOCKS):
+                blocks.append((s, c, h))
+
+    def carries_adj(s, h):
+        return s == HALVES - 1 and h == HALF_BLOCKS - 1
 
     with tc.manual_schedule(), tc.tile_pool(name="resident", bufs=1) as resident, tc.tile_pool(
-        name="raw", bufs=LOADS_AHEAD + 1
-    ) as raw_pool, tc.tile_pool(name="stream", bufs=3) as stream, tc.tile_pool(
+        name="raw", bufs=10
+    ) as raw_pool, tc.tile_pool(name="words", bufs=6) as words_pool, tc.tile_pool(
+        name="grouped", bufs=4
+    ) as grouped_pool, tc.tile_pool(name="operands", bufs=6) as operand_pool, tc.tile_pool(
         name="support", bufs=2
     ) as support_pool, tc.tile_pool(name="rows", bufs=4) as rows_pool:
         identity = resident.tile([P, P], F32)
         make_identity(nc, identity[:])
 
-        w_codes = resident.tile([P, CHUNKS * CHUNK_PASSES, HIDDEN], U32, align_bytes=64)
+        warm = resident.tile([P, 1], F32)
+        nc.vector.memset(warm[:], 0.0)
+        nc.scalar.activation(out=warm[:], in_=warm[:], func=mybir.ActivationFunctionType.Relu)
+
+        w_codes = resident.tile([P, FEATURES // K_PASS, HIDDEN], U32, align_bytes=64)
         w_scales = resident.tile([P, CHUNKS, HIDDEN], U8, align_bytes=64)
         nc.vector.memset(w_scales[:].bitcast(I32), 0)
 
@@ -56,14 +63,18 @@ def tile_gcn_pa_k_kernel(tc, x_init, adj1, W1_words, W1_scales, b1, out):
         support_scales = resident.tile([P, HALVES, HIDDEN], U8, align_bytes=64)
         bias = resident.tile([P, HIDDEN], BF16)
 
+        x_tiles = x_init.rearrange("(s p t) f -> s t p f", s=HALVES, t=PACK)
+        adj_pieces = adj1.rearrange("(c r i) k -> c r (i k)", r=P, i=PIECE_ROW_TILES)
+        out_tiles = out.rearrange("(c r i) n -> c i r n", r=P, i=PIECE_ROW_TILES)
+
         raw_of = {}
-        sorted_of = {}
-        codes_of = {}
+        words_of = {}
+        operands_of = {}
         support_sum = {}
-        support_rows = {}
+        support_grouped = {}
 
         def load_weight_chunk(c):
-            passes = slice(c * CHUNK_PASSES, (c + 1) * CHUNK_PASSES)
+            passes = slice(c * PIECE_SEGMENTS, (c + 1) * PIECE_SEGMENTS)
             for quadrant in range(4):
                 nc.sync.dma_start(
                     out=w_scales[32 * quadrant : 32 * quadrant + 16, c, :].bitcast(I32),
@@ -75,101 +86,97 @@ def tile_gcn_pa_k_kernel(tc, x_init, adj1, W1_words, W1_scales, b1, out):
             )
 
         def load(j):
-            kind, s, c, h = blocks[j]
-            raw = raw_pool.tile([P, SEGMENTS, K_PASS], BF16)
-            raw_of[j] = raw
-            if kind == "x":
-                tiles = slice(h * BLOCK_TILES, (h + 1) * BLOCK_TILES)
-                nc.sync.dma_start(
-                    out=raw[:].rearrange("p (t g) k -> p t (g k)", t=BLOCK_TILES),
-                    in_=x_init[s * K_PASS : (s + 1) * K_PASS, c * CHUNK : (c + 1) * CHUNK].rearrange(
-                        "(p t) f -> p t f", t=PACK
-                    )[:, tiles, :],
-                )
-                if s == 0 and h == PACK // BLOCK_TILES - 1:
-                    load_weight_chunk(c)
-            else:
-                nc.sync.dma_start(
-                    out=raw[:].rearrange("p s k -> p (s k)"),
-                    in_=adj1[s * K_PASS : (s + 1) * K_PASS, :].rearrange(
-                        "(p a) k -> p (a k)", a=ADJ_BLOCK_TILES
-                    ),
-                )
+            s, c, h = blocks[j]
+            sources = [
+                x_tiles[s, h * BLOCK_TILES + i, :, c * PIECE : (c + 1) * PIECE]
+                for i in range(BLOCK_TILES)
+            ]
+            if carries_adj(s, h):
+                sources.append(adj_pieces[c])
+            raw_of[j] = []
+            for source in sources:
+                raw = raw_pool.tile([P, PIECE_SEGMENTS, K_PASS], BF16)
+                nc.sync.dma_start(out=raw[:].rearrange("r s k -> r (s k)"), in_=source)
+                raw_of[j].append(raw)
+            if s == 0 and h == HALF_BLOCKS - 1:
+                load_weight_chunk(c)
 
         def sort_words(j):
-            words = stream.tile([P, SEGMENTS, 2, P], F32)
-            sorted_of[j] = words
-            nc.vector.tensor_copy(
-                out=words[:],
-                in_=raw_of[j][:].bitcast(F32).rearrange("r s (p u) -> r s u p", u=2),
-            )
+            words_of[j] = []
+            for raw in raw_of[j]:
+                words = words_pool.tile([P, PIECE_SEGMENTS, 2, P], F32)
+                nc.vector.tensor_copy(
+                    out=words[:], in_=raw[:].bitcast(F32).rearrange("r s (p u) -> r s u p", u=2)
+                )
+                words_of[j].append(words)
 
         def transpose_and_quantise(j):
-            kind, s, c, h = blocks[j]
-            grouped = stream.tile([P, SEGMENTS, P, PACK], BF16, align_bytes=64)
-            for bank in range(SEGMENTS // BANK_SEGMENTS):
-                first = bank * BANK_SEGMENTS
-                planes = transposed.tile([P, BANK_SEGMENTS, 2, P], F32)
-                for i in range(BANK_SEGMENTS):
-                    for u in range(2):
-                        nc.tensor.transpose(
-                            planes[:, i, u, :], sorted_of[j][:, first + i, u, :], identity[:]
-                        )
-                nc.scalar.copy(
-                    out=grouped[:, first : first + BANK_SEGMENTS, :, :].bitcast(F32),
-                    in_=planes[:].rearrange("p s u r -> p s r u"),
+            s, c, h = blocks[j]
+            operands_of[j] = []
+            for n, words in enumerate(words_of[j]):
+                grouped = grouped_pool.tile([P, PIECE_SEGMENTS, P, PACK], BF16, align_bytes=64)
+                for first in range(0, PIECE_SEGMENTS, BANK_SEGMENTS):
+                    planes = transposed.tile([P, BANK_SEGMENTS, 2, P], F32)
+                    for i in range(BANK_SEGMENTS):
+                        for u in range(2):
+                            nc.tensor.transpose(
+                                planes[:, i, u, :], words[:, first + i, u, :], identity[:]
+                            )
+                    nc.scalar.copy(
+                        out=grouped[:, first : first + BANK_SEGMENTS, :, :].bitcast(F32),
+                        in_=planes[:].rearrange("p s u r -> p s r u"),
+                    )
+                if n < BLOCK_TILES:
+                    codes_tile = operand_pool.tile([P, PIECE_SEGMENTS, P], U32, align_bytes=64)
+                    scales_tile = operand_pool.tile([P, PIECE_SEGMENTS, P], U8, align_bytes=64)
+                    codes, scales = codes_tile[:], scales_tile[:]
+                else:
+                    segments = slice(c * PIECE_SEGMENTS, (c + 1) * PIECE_SEGMENTS)
+                    codes, scales = adj_codes[:, segments, :], adj_scales[:, segments, :]
+                nc.vector.quantize_mx(
+                    out=codes.rearrange("p s r -> p (s r)").bitcast(FP8X4),
+                    scales=scales.rearrange("p s r -> p (s r)"),
+                    in_=grouped[:].rearrange("p s r t -> p (s r t)"),
                 )
-            if kind == "x":
-                codes = stream.tile([P, SEGMENTS, P], U32, align_bytes=64)
-                scales = stream.tile([P, SEGMENTS, P], U8, align_bytes=64)
-                codes_of[j] = (codes[:], scales[:])
-            else:
-                segments = slice(s * SEGMENTS, (s + 1) * SEGMENTS)
-                codes_of[j] = (adj_codes[:, segments, :], adj_scales[:, segments, :])
-            nc.vector.quantize_mx(
-                out=codes_of[j][0].rearrange("p s r -> p (s r)").bitcast(FP8X4),
-                scales=codes_of[j][1].rearrange("p s r -> p (s r)"),
-                in_=grouped[:].rearrange("p s r t -> p (s r t)"),
-            )
+                operands_of[j].append((codes, scales))
 
         def multiply(j):
-            kind, s, c, h = blocks[j]
-            if kind != "x":
-                return
-            codes, scales = codes_of[j]
+            s, c, h = blocks[j]
             for i in range(BLOCK_TILES):
                 t = h * BLOCK_TILES + i
+                codes, scales = operands_of[j][i]
                 if c == 0:
                     sums = sums_pool.tile([P, HIDDEN], F32, name="support_sum%d" % t)
                     support_sum[t] = sums
-                for g in range(CHUNK_PASSES):
+                for g in range(PIECE_SEGMENTS):
                     nc.tensor.matmul_mx(
                         out=support_sum[t][:],
-                        lhsT=codes[:, i * CHUNK_PASSES + g, :].bitcast(FP8X4),
-                        lhsT_scale=scales[:, i * CHUNK_PASSES + g, :],
-                        rhs=w_codes[:, c * CHUNK_PASSES + g, :].bitcast(FP8X4),
+                        lhsT=codes[:, g, :].bitcast(FP8X4),
+                        lhsT_scale=scales[:, g, :],
+                        rhs=w_codes[:, c * PIECE_SEGMENTS + g, :].bitcast(FP8X4),
                         rhs_scale=w_scales[4 * g : P, c, :],
                         start=(c == 0 and g == 0),
-                        stop=(c == CHUNKS - 1 and g == CHUNK_PASSES - 1),
+                        stop=(c == CHUNKS - 1 and g == PIECE_SEGMENTS - 1),
                     )
             if c == CHUNKS - 1:
                 quantise_support(s, h)
 
         def quantise_support(s, h):
+            tiles = slice(h * BLOCK_TILES, (h + 1) * BLOCK_TILES)
             if h == 0:
-                rounded = support_pool.tile([P, PACK, HIDDEN], BF16)
-                support_rows[s] = rounded
-            for t in range(h * BLOCK_TILES, (h + 1) * BLOCK_TILES):
-                nc.scalar.copy(out=support_rows[s][:, t, :], in_=support_sum[t][:])
-            if h == PACK // BLOCK_TILES - 1:
                 grouped = support_pool.tile([P, HIDDEN, PACK], BF16, align_bytes=64)
-                nc.vector.tensor_copy(
-                    out=grouped[:], in_=support_rows[s][:].rearrange("p t n -> p n t")
-                )
+                support_grouped[s] = grouped
+            rounded = support_pool.tile([P, BLOCK_TILES, HIDDEN], BF16)
+            for i in range(BLOCK_TILES):
+                nc.scalar.copy(out=rounded[:, i, :], in_=support_sum[h * BLOCK_TILES + i][:])
+            nc.vector.tensor_copy(
+                out=support_grouped[s][:, :, tiles], in_=rounded[:].rearrange("p t n -> p n t")
+            )
+            if h == HALF_BLOCKS - 1:
                 nc.vector.quantize_mx(
                     out=support_codes[:, s, :].bitcast(FP8X4),
                     scales=support_scales[:, s, :],
-                    in_=grouped[:].rearrange("p n t -> p (n t)"),
+                    in_=support_grouped[s][:].rearrange("p n t -> p (n t)"),
                 )
 
         with tc.psum_pool(name="transposed", bufs=4) as transposed, tc.psum_pool(
@@ -187,7 +194,6 @@ def tile_gcn_pa_k_kernel(tc, x_init, adj1, W1_words, W1_scales, b1, out):
 
         nc.sync.dma_start(out=bias[:], in_=b1.partition_broadcast(P))
 
-        out_tiles = out.rearrange("(b r i) n -> b i r n", r=P, i=ADJ_BLOCK_TILES)
         with tc.psum_pool(name="y", bufs=ROW_TILES, reuse_waits="tile") as y_pool:
             y_sums = []
             for a in range(ROW_TILES):
@@ -213,5 +219,5 @@ def tile_gcn_pa_k_kernel(tc, x_init, adj1, W1_words, W1_scales, b1, out):
                     out=y_rows[:], in_=y_rows[:], func=mybir.ActivationFunctionType.Relu
                 )
                 nc.sync.dma_start(
-                    out=out_tiles[a // ADJ_BLOCK_TILES, a % ADJ_BLOCK_TILES], in_=y_rows[:]
+                    out=out_tiles[a // PIECE_ROW_TILES, a % PIECE_ROW_TILES], in_=y_rows[:]
                 )

@@ -45,7 +45,7 @@ def tile_gcn_pa_k_kernel(tc, x_init, adj1, W1_words, W1_scales, b1, out):
         name="grouped", bufs=4
     ) as grouped_pool, tc.tile_pool(name="operands", bufs=6) as operand_pool, tc.tile_pool(
         name="support", bufs=2
-    ) as support_pool, tc.tile_pool(name="rows", bufs=4) as rows_pool:
+    ) as support_pool, tc.tile_pool(name="rows", bufs=ROW_TILES) as rows_pool:
         identity = resident.tile([P, P], F32)
         make_identity(nc, identity[:])
 

@@ -22,6 +22,8 @@ BLOCK_TILES = 2
 HALF_BLOCKS = PACK // BLOCK_TILES
 ROW_TILES = NODES // P
 PIECE_ROW_TILES = PIECE // NODES
+SIDES = 2
+SIDE = HIDDEN // SIDES
 LOADS_AHEAD = 3
 
 FLOPS = 2 * NODES * FEATURES * HIDDEN + 2 * NODES * NODES * HIDDEN
@@ -31,19 +33,21 @@ def tile_gcn_pa_k_kernel(tc, x_init, adj1, W1_words, W1_scales, b1, out):
     nc = tc.nc
 
     blocks = []
-    for s in range(HALVES):
+    for c in range(CHUNKS):
+        for h in range(HALF_BLOCKS):
+            blocks.append((0, (2 * h, 2 * h + 1), c, None))
+    for h in range(HALF_BLOCKS):
         for c in range(CHUNKS):
-            for h in range(HALF_BLOCKS):
-                blocks.append((s, c, h))
-
-    def carries_adj(s, h):
-        return s == HALVES - 1 and h == HALF_BLOCKS - 1
+            blocks.append((1, (2 * h, 2 * h + 1), c, c if h == 0 else None))
+    late_blocks = list(range(len(blocks) - CHUNKS, len(blocks)))
 
     with tc.manual_schedule(), tc.tile_pool(name="resident", bufs=1) as resident, tc.tile_pool(
         name="raw", bufs=10
     ) as raw_pool, tc.tile_pool(name="words", bufs=6) as words_pool, tc.tile_pool(
         name="grouped", bufs=4
     ) as grouped_pool, tc.tile_pool(name="operands", bufs=6) as operand_pool, tc.tile_pool(
+        name="late", bufs=CHUNKS * BLOCK_TILES
+    ) as late_pool, tc.tile_pool(
         name="support", bufs=2
     ) as support_pool, tc.tile_pool(name="rows", bufs=ROW_TILES) as rows_pool:
         identity = resident.tile([P, P], F32)
@@ -62,10 +66,11 @@ def tile_gcn_pa_k_kernel(tc, x_init, adj1, W1_words, W1_scales, b1, out):
         support_codes = resident.tile([P, HALVES, HIDDEN], U32, align_bytes=64)
         support_scales = resident.tile([P, HALVES, HIDDEN], U8, align_bytes=64)
         bias = resident.tile([P, HIDDEN], BF16)
+        bias_pairs = resident.tile([P, SIDES, PIECE_ROW_TILES, SIDE], BF16)
 
         x_tiles = x_init.rearrange("(s p t) f -> s t p f", s=HALVES, t=PACK)
         adj_pieces = adj1.rearrange("(c r i) k -> c r (i k)", r=P, i=PIECE_ROW_TILES)
-        out_tiles = out.rearrange("(c r i) n -> c i r n", r=P, i=PIECE_ROW_TILES)
+        out_pairs = out.rearrange("(c r i) n -> c r i n", r=P, i=PIECE_ROW_TILES)
 
         raw_of = {}
         words_of = {}
@@ -86,19 +91,16 @@ def tile_gcn_pa_k_kernel(tc, x_init, adj1, W1_words, W1_scales, b1, out):
             )
 
         def load(j):
-            s, c, h = blocks[j]
-            sources = [
-                x_tiles[s, h * BLOCK_TILES + i, :, c * PIECE : (c + 1) * PIECE]
-                for i in range(BLOCK_TILES)
-            ]
-            if carries_adj(s, h):
-                sources.append(adj_pieces[c])
+            s, tiles, c, adj_piece = blocks[j]
+            sources = [x_tiles[s, t, :, c * PIECE : (c + 1) * PIECE] for t in tiles]
+            if adj_piece is not None:
+                sources.append(adj_pieces[adj_piece])
             raw_of[j] = []
             for source in sources:
                 raw = raw_pool.tile([P, PIECE_SEGMENTS, K_PASS], BF16)
                 nc.sync.dma_start(out=raw[:].rearrange("r s k -> r (s k)"), in_=source)
                 raw_of[j].append(raw)
-            if s == 0 and h == HALF_BLOCKS - 1:
+            if s == 0 and tiles[-1] == PACK - 1:
                 load_weight_chunk(c)
 
         def sort_words(j):
@@ -111,12 +113,12 @@ def tile_gcn_pa_k_kernel(tc, x_init, adj1, W1_words, W1_scales, b1, out):
                 words_of[j].append(words)
 
         def transpose_and_quantise(j):
-            s, c, h = blocks[j]
+            adj_piece = blocks[j][3]
             operands_of[j] = []
             for n, words in enumerate(words_of[j]):
                 grouped = grouped_pool.tile([P, PIECE_SEGMENTS, P, PACK], BF16, align_bytes=64)
                 for first in range(0, PIECE_SEGMENTS, BANK_SEGMENTS):
-                    planes = transposed.tile([P, BANK_SEGMENTS, 2, P], F32)
+                    planes = transposed.tile([P, BANK_SEGMENTS, 2, P], F32, name="planes")
                     for i in range(BANK_SEGMENTS):
                         for u in range(2):
                             nc.tensor.transpose(
@@ -127,11 +129,12 @@ def tile_gcn_pa_k_kernel(tc, x_init, adj1, W1_words, W1_scales, b1, out):
                         in_=planes[:].rearrange("p s u r -> p s r u"),
                     )
                 if n < BLOCK_TILES:
-                    codes_tile = operand_pool.tile([P, PIECE_SEGMENTS, P], U32, align_bytes=64)
-                    scales_tile = operand_pool.tile([P, PIECE_SEGMENTS, P], U8, align_bytes=64)
+                    pool = late_pool if j in late_blocks else operand_pool
+                    codes_tile = pool.tile([P, PIECE_SEGMENTS, P], U32, align_bytes=64, name="codes")
+                    scales_tile = pool.tile([P, PIECE_SEGMENTS, P], U8, align_bytes=64, name="scales")
                     codes, scales = codes_tile[:], scales_tile[:]
                 else:
-                    segments = slice(c * PIECE_SEGMENTS, (c + 1) * PIECE_SEGMENTS)
+                    segments = slice(adj_piece * PIECE_SEGMENTS, (adj_piece + 1) * PIECE_SEGMENTS)
                     codes, scales = adj_codes[:, segments, :], adj_scales[:, segments, :]
                 nc.vector.quantize_mx(
                     out=codes.rearrange("p s r -> p (s r)").bitcast(FP8X4),
@@ -140,84 +143,131 @@ def tile_gcn_pa_k_kernel(tc, x_init, adj1, W1_words, W1_scales, b1, out):
                 )
                 operands_of[j].append((codes, scales))
 
-        def multiply(j):
-            s, c, h = blocks[j]
-            for i in range(BLOCK_TILES):
-                t = h * BLOCK_TILES + i
-                codes, scales = operands_of[j][i]
-                if c == 0:
-                    sums = sums_pool.tile([P, HIDDEN], F32, name="support_sum%d" % t)
-                    support_sum[t] = sums
-                for g in range(PIECE_SEGMENTS):
-                    nc.tensor.matmul_mx(
-                        out=support_sum[t][:],
-                        lhsT=codes[:, g, :].bitcast(FP8X4),
-                        lhsT_scale=scales[:, g, :],
-                        rhs=w_codes[:, c * PIECE_SEGMENTS + g, :].bitcast(FP8X4),
-                        rhs_scale=w_scales[4 * g : P, c, :],
-                        start=(c == 0 and g == 0),
-                        stop=(c == CHUNKS - 1 and g == PIECE_SEGMENTS - 1),
-                    )
-            if c == CHUNKS - 1:
-                quantise_support(s, h)
-
-        def quantise_support(s, h):
-            tiles = slice(h * BLOCK_TILES, (h + 1) * BLOCK_TILES)
-            if h == 0:
-                grouped = support_pool.tile([P, HIDDEN, PACK], BF16, align_bytes=64)
-                support_grouped[s] = grouped
-            rounded = support_pool.tile([P, BLOCK_TILES, HIDDEN], BF16)
-            for i in range(BLOCK_TILES):
-                nc.scalar.copy(out=rounded[:, i, :], in_=support_sum[h * BLOCK_TILES + i][:])
-            nc.vector.tensor_copy(
-                out=support_grouped[s][:, :, tiles], in_=rounded[:].rearrange("p t n -> p n t")
-            )
-            if h == HALF_BLOCKS - 1:
-                nc.vector.quantize_mx(
-                    out=support_codes[:, s, :].bitcast(FP8X4),
-                    scales=support_scales[:, s, :],
-                    in_=support_grouped[s][:].rearrange("p n t -> p (n t)"),
+        def multiply(j, i, first_column, width, bank):
+            s, tiles, c, adj_piece = blocks[j]
+            codes, scales = operands_of[j][i]
+            columns = slice(first_column, first_column + width)
+            key = (s, tiles[i], first_column)
+            if c == 0:
+                sums = sums_pool.tile([P, HIDDEN], F32, name="sums%d" % bank)
+                support_sum[key] = sums
+            for g in range(PIECE_SEGMENTS):
+                nc.tensor.matmul_mx(
+                    out=support_sum[key][:, 0:width],
+                    lhsT=codes[:, g, :].bitcast(FP8X4),
+                    lhsT_scale=scales[:, g, :],
+                    rhs=w_codes[:, c * PIECE_SEGMENTS + g, columns].bitcast(FP8X4),
+                    rhs_scale=w_scales[4 * g : P, c, columns],
+                    start=(c == 0 and g == 0),
+                    stop=(c == CHUNKS - 1 and g == PIECE_SEGMENTS - 1),
                 )
+
+        def group_support(s, first_tile, first_column, width):
+            if first_tile == 0:
+                grouped = support_pool.tile([P, HIDDEN, PACK], BF16, align_bytes=64, name="support_grouped")
+                support_grouped[s] = grouped
+            rounded = support_pool.tile([P, BLOCK_TILES, HIDDEN], BF16, name="rounded")
+            for i in range(BLOCK_TILES):
+                nc.scalar.copy(
+                    out=rounded[:, i, 0:width],
+                    in_=support_sum[s, first_tile + i, first_column][:, 0:width],
+                )
+            nc.vector.tensor_copy(
+                out=support_grouped[s][
+                    :, first_column : first_column + width, first_tile : first_tile + BLOCK_TILES
+                ],
+                in_=rounded[:, :, 0:width].rearrange("p t n -> p n t"),
+            )
+
+        def quantise_support(s, first_column, width):
+            columns = slice(first_column, first_column + width)
+            nc.vector.quantize_mx(
+                out=support_codes[:, s, columns].bitcast(FP8X4),
+                scales=support_scales[:, s, columns],
+                in_=support_grouped[s][:, columns, :].rearrange("p n t -> p (n t)"),
+            )
+
+        def multiply_block(j):
+            s, tiles, c, adj_piece = blocks[j]
+            late = j in late_blocks
+            for i in range(BLOCK_TILES):
+                multiply(j, i, 0, SIDE if late else HIDDEN, tiles[i])
+            if c == CHUNKS - 1 and not late:
+                group_support(s, tiles[0], 0, HIDDEN)
+                if tiles[-1] == PACK - 1:
+                    quantise_support(s, 0, HIDDEN)
+
+        y_rows = {}
+
+        def multiply_adj(side, c):
+            columns = slice(side * SIDE, (side + 1) * SIDE)
+            if side == 0:
+                bank = transposed.tile([P, BANK_SEGMENTS, 2, P], F32, name="planes")
+                y_sums = bank[:].rearrange("p i u r -> p i (u r)")
+            else:
+                bank = sums_pool.tile([P, HIDDEN], F32, name="sums%d" % ((2, 3, 0, 1)[c]))
+                y_sums = bank[:].rearrange("p (i n) -> p i n", i=PIECE_ROW_TILES)
+            for i in range(PIECE_ROW_TILES):
+                for s in range(HALVES):
+                    segment = (c * PIECE_ROW_TILES + i) * HALVES + s
+                    nc.tensor.matmul_mx(
+                        out=y_sums[:, i, :],
+                        lhsT=adj_codes[:, segment, :].bitcast(FP8X4),
+                        lhsT_scale=adj_scales[:, segment, :],
+                        rhs=support_codes[:, s, columns].bitcast(FP8X4),
+                        rhs_scale=support_scales[:, s, columns],
+                        start=(s == 0),
+                        stop=(s == HALVES - 1),
+                    )
+            y_rows[side, c] = y_sums
+
+        def finish_rows(side, c):
+            rows = rows_pool.tile([P, PIECE_ROW_TILES, SIDE], F32)
+            nc.vector.tensor_tensor(
+                out=rows[:], in0=y_rows[side, c], in1=bias_pairs[:, side, :, :], op=mybir.AluOpType.add
+            )
+            nc.scalar.activation(
+                out=rows[:], in_=rows[:], func=mybir.ActivationFunctionType.Relu
+            )
+            nc.sync.dma_start(
+                out=out_pairs[c, :, :, side * SIDE : (side + 1) * SIDE], in_=rows[:]
+            )
 
         with tc.psum_pool(name="transposed", bufs=4) as transposed, tc.psum_pool(
             name="sums", bufs=1
         ) as sums_pool:
-            for step in range(len(blocks) + LOADS_AHEAD + 2):
+            for step in range(len(blocks) + LOADS_AHEAD + 1):
                 if step < len(blocks):
                     load(step)
+                if step == len(blocks):
+                    nc.sync.dma_start(out=bias[:], in_=b1.partition_broadcast(P))
                 if 0 <= step - LOADS_AHEAD < len(blocks):
                     sort_words(step - LOADS_AHEAD)
                 if 0 <= step - LOADS_AHEAD - 1 < len(blocks):
                     transpose_and_quantise(step - LOADS_AHEAD - 1)
                 if 0 <= step - LOADS_AHEAD - 2 < len(blocks):
-                    multiply(step - LOADS_AHEAD - 2)
+                    multiply_block(step - LOADS_AHEAD - 2)
 
-        nc.sync.dma_start(out=bias[:], in_=b1.partition_broadcast(P))
-
-        with tc.psum_pool(name="y", bufs=ROW_TILES, reuse_waits="tile") as y_pool:
-            y_sums = []
-            for a in range(ROW_TILES):
-                y_sum = y_pool.tile([P, HIDDEN], F32)
-                y_sums.append(y_sum)
-            for s in range(HALVES):
-                for a in range(ROW_TILES):
-                    nc.tensor.matmul_mx(
-                        out=y_sums[a][:],
-                        lhsT=adj_codes[:, a * HALVES + s, :].bitcast(FP8X4),
-                        lhsT_scale=adj_scales[:, a * HALVES + s, :],
-                        rhs=support_codes[:, s, :].bitcast(FP8X4),
-                        rhs_scale=support_scales[:, s, :],
-                        start=(s == 0),
-                        stop=(s == HALVES - 1),
-                    )
-            for a in range(ROW_TILES):
-                y_rows = rows_pool.tile([P, HIDDEN], F32)
-                nc.vector.tensor_tensor(
-                    out=y_rows[:], in0=y_sums[a][:], in1=bias[:], op=mybir.AluOpType.add
+            for i in range(PIECE_ROW_TILES):
+                nc.vector.tensor_copy(
+                    out=bias_pairs[:, :, i, :], in_=bias[:].rearrange("p (h n) -> p h n", h=SIDES)
                 )
-                nc.scalar.activation(
-                    out=y_rows[:], in_=y_rows[:], func=mybir.ActivationFunctionType.Relu
-                )
-                nc.sync.dma_start(
-                    out=out_tiles[a // PIECE_ROW_TILES, a % PIECE_ROW_TILES], in_=y_rows[:]
-                )
+            for j in late_blocks[:-1]:
+                multiply(j, 0, SIDE, SIDE, 0)
+            multiply_block(late_blocks[-1])
+            group_support(1, 2, 0, SIDE)
+            quantise_support(1, 0, SIDE)
+            multiply(late_blocks[-1], 0, SIDE, SIDE, 0)
+            for j in late_blocks:
+                multiply(j, 1, SIDE, SIDE, 1)
+            for c in range(CHUNKS):
+                multiply_adj(0, c)
+            finish_rows(0, 0)
+            group_support(1, 2, SIDE, SIDE)
+            quantise_support(1, SIDE, SIDE)
+            for c in range(1, CHUNKS):
+                finish_rows(0, c)
+            for c in range(CHUNKS):
+                multiply_adj(1, c)
+            for c in range(CHUNKS):
+                finish_rows(1, c)

@@ -42,7 +42,7 @@ def tile_gcn_pa_k_kernel(tc, x_init, adj1, W1_words, W1_scales, b1, out):
     late_blocks = list(range(len(blocks) - CHUNKS, len(blocks)))
 
     with tc.manual_schedule(), tc.tile_pool(name="resident", bufs=1) as resident, tc.tile_pool(
-        name="raw", bufs=10
+        name="raw", bufs=12
     ) as raw_pool, tc.tile_pool(name="words", bufs=6) as words_pool, tc.tile_pool(
         name="grouped", bufs=4
     ) as grouped_pool, tc.tile_pool(name="operands", bufs=6) as operand_pool, tc.tile_pool(
@@ -262,10 +262,9 @@ def tile_gcn_pa_k_kernel(tc, x_init, adj1, W1_words, W1_scales, b1, out):
                 multiply(j, 1, SIDE, SIDE, 1)
             for c in range(CHUNKS):
                 multiply_adj(0, c)
-            finish_rows(0, 0)
             group_support(1, 2, SIDE, SIDE)
             quantise_support(1, SIDE, SIDE)
-            for c in range(1, CHUNKS):
+            for c in range(CHUNKS):
                 finish_rows(0, c)
             for c in range(CHUNKS):
                 multiply_adj(1, c)

@@ -20,11 +20,16 @@ CHUNKS = FEATURES // PIECE
 BANK_SEGMENTS = 2
 BLOCK_TILES = 2
 HALF_BLOCKS = PACK // BLOCK_TILES
+PASSES = FEATURES // K_PASS
 ROW_TILES = NODES // P
 PIECE_ROW_TILES = PIECE // NODES
 SIDES = 2
 SIDE = HIDDEN // SIDES
-LOADS_AHEAD = 3
+RAW_PIECES = 12
+SORT_AHEAD = 2
+BANKS_PER_PIECE = PIECE_SEGMENTS // BANK_SEGMENTS
+RUN_BANKS = 4
+LAG_BANKS = 4
 
 FLOPS = 2 * NODES * FEATURES * HIDDEN + 2 * NODES * NODES * HIDDEN
 
@@ -32,20 +37,36 @@ FLOPS = 2 * NODES * FEATURES * HIDDEN + 2 * NODES * NODES * HIDDEN
 def tile_gcn_pa_k_kernel(tc, x_init, adj1, W1_words, W1_scales, b1, out):
     nc = tc.nc
 
-    blocks = []
+    def x_piece(s, tiles, passes):
+        return (s, [(t, g) for t in tiles for g in passes])
+
+    def chunk_passes(c):
+        return range(c * PIECE_SEGMENTS, (c + 1) * PIECE_SEGMENTS)
+
+    pieces = []
+    weight_after = {}
+    for g in range(4):
+        pieces.append(x_piece(0, range(PACK), [g]))
+        weight_after[len(pieces) - 1] = (g, 1)
+    for c in range(1, CHUNKS):
+        for t in range(PACK):
+            pieces.append(x_piece(0, [t], chunk_passes(c)))
+        weight_after[len(pieces) - 1] = (c * PIECE_SEGMENTS, PIECE_SEGMENTS)
     for c in range(CHUNKS):
-        for h in range(HALF_BLOCKS):
-            blocks.append((0, (2 * h, 2 * h + 1), c, None))
-    for h in range(HALF_BLOCKS):
-        for c in range(CHUNKS):
-            blocks.append((1, (2 * h, 2 * h + 1), c, c if h == 0 else None))
-    late_blocks = list(range(len(blocks) - CHUNKS, len(blocks)))
+        for t in range(BLOCK_TILES):
+            pieces.append(x_piece(1, [t], chunk_passes(c)))
+        pieces.append((None, c))
+    first_late = len(pieces)
+    first_deferred = first_late + (CHUNKS - 2) * BLOCK_TILES
+    for c in range(CHUNKS):
+        for t in range(BLOCK_TILES, PACK):
+            pieces.append(x_piece(1, [t], chunk_passes(c)))
 
     with tc.manual_schedule(), tc.tile_pool(name="resident", bufs=1) as resident, tc.tile_pool(
-        name="raw", bufs=12
-    ) as raw_pool, tc.tile_pool(name="words", bufs=6) as words_pool, tc.tile_pool(
+        name="raw", bufs=RAW_PIECES
+    ) as raw_pool, tc.tile_pool(name="words", bufs=5) as words_pool, tc.tile_pool(
         name="grouped", bufs=4
-    ) as grouped_pool, tc.tile_pool(name="operands", bufs=6) as operand_pool, tc.tile_pool(
+    ) as grouped_pool, tc.tile_pool(name="operands", bufs=8) as operand_pool, tc.tile_pool(
         name="late", bufs=CHUNKS * BLOCK_TILES
     ) as late_pool, tc.tile_pool(
         name="support", bufs=2
@@ -57,6 +78,8 @@ def tile_gcn_pa_k_kernel(tc, x_init, adj1, W1_words, W1_scales, b1, out):
         nc.vector.memset(warm[:], 0.0)
         nc.scalar.activation(out=warm[:], in_=warm[:], func=mybir.ActivationFunctionType.Relu)
 
+        zeros = resident.tile([P, HIDDEN], BF16)
+        nc.vector.memset(zeros[:].bitcast(I32), 0)
         w_codes = resident.tile([P, FEATURES // K_PASS, HIDDEN], U32, align_bytes=64)
         w_scales = resident.tile([P, CHUNKS, HIDDEN], U8, align_bytes=64)
         nc.vector.memset(w_scales[:].bitcast(I32), 0)
@@ -68,98 +91,131 @@ def tile_gcn_pa_k_kernel(tc, x_init, adj1, W1_words, W1_scales, b1, out):
         bias = resident.tile([P, HIDDEN], BF16)
         bias_pairs = resident.tile([P, SIDES, PIECE_ROW_TILES, SIDE], BF16)
 
-        x_tiles = x_init.rearrange("(s p t) f -> s t p f", s=HALVES, t=PACK)
+        x_rows = x_init.rearrange("(s p t) f -> s p t f", s=HALVES, t=PACK)
         adj_pieces = adj1.rearrange("(c r i) k -> c r (i k)", r=P, i=PIECE_ROW_TILES)
         out_pairs = out.rearrange("(c r i) n -> c r i n", r=P, i=PIECE_ROW_TILES)
 
         raw_of = {}
         words_of = {}
+        grouped_of = {}
         operands_of = {}
         support_sum = {}
         support_grouped = {}
 
-        def load_weight_chunk(c):
+        def load_scales(c):
             passes = slice(c * PIECE_SEGMENTS, (c + 1) * PIECE_SEGMENTS)
             for quadrant in range(4):
                 nc.sync.dma_start(
                     out=w_scales[32 * quadrant : 32 * quadrant + 16, c, :].bitcast(I32),
                     in_=W1_scales[passes, 4 * quadrant : 4 * quadrant + 4, :].bitcast(I32),
                 )
+
+        def load_weight(first, count):
+            passes = slice(first, first + count)
             nc.sync.dma_start(
                 out=w_codes[:, passes, :].bitcast(I32),
                 in_=W1_words[passes].rearrange("g p n t -> p g (n t)").bitcast(I32),
             )
 
-        def load(j):
-            s, tiles, c, adj_piece = blocks[j]
-            sources = [x_tiles[s, t, :, c * PIECE : (c + 1) * PIECE] for t in tiles]
-            if adj_piece is not None:
-                sources.append(adj_pieces[adj_piece])
-            raw_of[j] = []
-            for source in sources:
-                raw = raw_pool.tile([P, PIECE_SEGMENTS, K_PASS], BF16)
-                nc.sync.dma_start(out=raw[:].rearrange("r s k -> r (s k)"), in_=source)
-                raw_of[j].append(raw)
-            if s == 0 and tiles[-1] == PACK - 1:
-                load_weight_chunk(c)
-
-        def sort_words(j):
-            words_of[j] = []
-            for raw in raw_of[j]:
-                words = words_pool.tile([P, PIECE_SEGMENTS, 2, P], F32)
-                nc.vector.tensor_copy(
-                    out=words[:], in_=raw[:].bitcast(F32).rearrange("r s (p u) -> r s u p", u=2)
+        def load(n):
+            s, segments = pieces[n]
+            raw = raw_pool.tile([P, PIECE_SEGMENTS, K_PASS], BF16)
+            if s is None:
+                nc.sync.dma_start(
+                    out=raw[:].rearrange("r s k -> r (s k)"), in_=adj_pieces[segments]
                 )
-                words_of[j].append(words)
-
-        def transpose_and_quantise(j):
-            adj_piece = blocks[j][3]
-            operands_of[j] = []
-            for n, words in enumerate(words_of[j]):
-                grouped = grouped_pool.tile([P, PIECE_SEGMENTS, P, PACK], BF16, align_bytes=64)
-                for first in range(0, PIECE_SEGMENTS, BANK_SEGMENTS):
-                    planes = transposed.tile([P, BANK_SEGMENTS, 2, P], F32, name="planes")
-                    for i in range(BANK_SEGMENTS):
-                        for u in range(2):
-                            nc.tensor.transpose(
-                                planes[:, i, u, :], words[:, first + i, u, :], identity[:]
-                            )
-                    nc.scalar.copy(
-                        out=grouped[:, first : first + BANK_SEGMENTS, :, :].bitcast(F32),
-                        in_=planes[:].rearrange("p s u r -> p s r u"),
+            else:
+                tiles = [t for t, g in segments]
+                passes = [g for t, g in segments]
+                first, last = min(passes), max(passes)
+                count = last + 1 - first
+                parts = 2 if n == 0 else 1
+                step = PIECE_SEGMENTS // parts
+                for i in range(0, PIECE_SEGMENTS, step):
+                    part_tiles = tiles[i : i + step]
+                    nc.sync.dma_start(
+                        out=raw[:, i : i + step, :].rearrange("r (t g) k -> r t (g k)", g=count),
+                        in_=x_rows[
+                            s, :, part_tiles[0] : part_tiles[-1] + 1, first * K_PASS : (last + 1) * K_PASS
+                        ],
                     )
-                if n < BLOCK_TILES:
-                    pool = late_pool if j in late_blocks else operand_pool
-                    codes_tile = pool.tile([P, PIECE_SEGMENTS, P], U32, align_bytes=64, name="codes")
-                    scales_tile = pool.tile([P, PIECE_SEGMENTS, P], U8, align_bytes=64, name="scales")
-                    codes, scales = codes_tile[:], scales_tile[:]
-                else:
-                    segments = slice(adj_piece * PIECE_SEGMENTS, (adj_piece + 1) * PIECE_SEGMENTS)
-                    codes, scales = adj_codes[:, segments, :], adj_scales[:, segments, :]
-                nc.vector.quantize_mx(
-                    out=codes.rearrange("p s r -> p (s r)").bitcast(FP8X4),
-                    scales=scales.rearrange("p s r -> p (s r)"),
-                    in_=grouped[:].rearrange("p s r t -> p (s r t)"),
-                )
-                operands_of[j].append((codes, scales))
+            raw_of[n] = raw
+            if n in weight_after:
+                first, count = weight_after[n]
+                if count == PIECE_SEGMENTS:
+                    load_scales(first // PIECE_SEGMENTS)
+                load_weight(first, count)
+            if n == 1:
+                load_scales(0)
+            if n == len(pieces) - 1:
+                nc.sync.dma_start(out=bias[:], in_=b1.partition_broadcast(P))
 
-        def multiply(j, i, first_column, width, bank):
-            s, tiles, c, adj_piece = blocks[j]
-            codes, scales = operands_of[j][i]
+        def sort_words(n):
+            words = words_pool.tile([P, PIECE_SEGMENTS, 2, P], F32)
+            step = BANK_SEGMENTS if n == 0 else PIECE_SEGMENTS
+            for first in range(0, PIECE_SEGMENTS, step):
+                nc.vector.tensor_copy(
+                    out=words[:, first : first + step, :, :],
+                    in_=raw_of[n][:, first : first + step, :]
+                    .bitcast(F32)
+                    .rearrange("r s (p u) -> r s u p", u=2),
+                )
+            words_of[n] = words
+
+        def transpose_bank(b):
+            n, i = divmod(b, BANKS_PER_PIECE)
+            if i == 0:
+                grouped = grouped_pool.tile([P, PIECE_SEGMENTS, P, PACK], BF16, align_bytes=64)
+                grouped_of[n] = grouped
+            first = i * BANK_SEGMENTS
+            planes = transposed.tile([P, BANK_SEGMENTS, 2, P], F32, name="planes")
+            for k in range(BANK_SEGMENTS):
+                for u in range(2):
+                    nc.tensor.transpose(
+                        planes[:, k, u, :], words_of[n][:, first + k, u, :], identity[:]
+                    )
+            nc.scalar.copy(
+                out=grouped_of[n][:, first : first + BANK_SEGMENTS, :, :].bitcast(F32),
+                in_=planes[:].rearrange("p s u r -> p s r u"),
+            )
+            if i == BANKS_PER_PIECE - 1:
+                quantise(n)
+
+        def quantise(n):
+            s, segments = pieces[n]
+            if s is None:
+                chunk = slice(segments * PIECE_SEGMENTS, (segments + 1) * PIECE_SEGMENTS)
+                codes, scales = adj_codes[:, chunk, :], adj_scales[:, chunk, :]
+            else:
+                pool = late_pool if n >= first_late else operand_pool
+                codes_tile = pool.tile([P, PIECE_SEGMENTS, P], U32, align_bytes=64, name="codes")
+                scales_tile = pool.tile([P, PIECE_SEGMENTS, P], U8, align_bytes=64, name="scales")
+                codes, scales = codes_tile[:], scales_tile[:]
+            nc.vector.quantize_mx(
+                out=codes.rearrange("p s r -> p (s r)").bitcast(FP8X4),
+                scales=scales.rearrange("p s r -> p (s r)"),
+                in_=grouped_of[n][:].rearrange("p s r t -> p (s r t)"),
+            )
+            operands_of[n] = (codes, scales)
+
+        def multiply(n, first, last, first_column, width, banks):
+            s, segments = pieces[n]
+            codes, scales = operands_of[n]
             columns = slice(first_column, first_column + width)
-            key = (s, tiles[i], first_column)
-            if c == 0:
-                sums = sums_pool.tile([P, HIDDEN], F32, name="sums%d" % bank)
-                support_sum[key] = sums
-            for g in range(PIECE_SEGMENTS):
+            for i in range(first, last):
+                t, g = segments[i]
+                key = (s, t, first_column)
+                if g == 0:
+                    sums = sums_pool.tile([P, HIDDEN], F32, name="sums%d" % banks[t])
+                    support_sum[key] = sums
                 nc.tensor.matmul_mx(
                     out=support_sum[key][:, 0:width],
-                    lhsT=codes[:, g, :].bitcast(FP8X4),
-                    lhsT_scale=scales[:, g, :],
-                    rhs=w_codes[:, c * PIECE_SEGMENTS + g, columns].bitcast(FP8X4),
-                    rhs_scale=w_scales[4 * g : P, c, columns],
-                    start=(c == 0 and g == 0),
-                    stop=(c == CHUNKS - 1 and g == PIECE_SEGMENTS - 1),
+                    lhsT=codes[:, i, :].bitcast(FP8X4),
+                    lhsT_scale=scales[:, i, :],
+                    rhs=w_codes[:, g, columns].bitcast(FP8X4),
+                    rhs_scale=w_scales[4 * (g % PIECE_SEGMENTS) : P, g // PIECE_SEGMENTS, columns],
+                    start=(g == 0),
+                    stop=(g == PASSES - 1),
                 )
 
         def group_support(s, first_tile, first_column, width):
@@ -187,17 +243,24 @@ def tile_gcn_pa_k_kernel(tc, x_init, adj1, W1_words, W1_scales, b1, out):
                 in_=support_grouped[s][:, columns, :].rearrange("p n t -> p (n t)"),
             )
 
-        def multiply_block(j):
-            s, tiles, c, adj_piece = blocks[j]
-            late = j in late_blocks
-            for i in range(BLOCK_TILES):
-                multiply(j, i, 0, SIDE if late else HIDDEN, tiles[i])
-            if c == CHUNKS - 1 and not late:
-                group_support(s, tiles[0], 0, HIDDEN)
-                if tiles[-1] == PACK - 1:
-                    quantise_support(s, 0, HIDDEN)
+        def multiply_bank(b):
+            n, i = divmod(b, BANKS_PER_PIECE)
+            s, segments = pieces[n]
+            if s is None:
+                return
+            late = n >= first_late
+            first = i * BANK_SEGMENTS
+            multiply(n, first, first + BANK_SEGMENTS, 0, SIDE if late else HIDDEN, range(PACK))
+            if late and n < first_deferred:
+                multiply(n, first, first + BANK_SEGMENTS, SIDE, SIDE, late_banks)
+            t, g = segments[first + BANK_SEGMENTS - 1]
+            if g == PASSES - 1 and t % BLOCK_TILES == BLOCK_TILES - 1 and not late:
+                group_support(s, t + 1 - BLOCK_TILES, 0, HIDDEN)
+                if t == PACK - 1:
+                    quantise_support(0, 0, HIDDEN)
 
         y_rows = {}
+        late_banks = {2: 0, 3: 1}
 
         def multiply_adj(side, c):
             columns = slice(side * SIDE, (side + 1) * SIDE)
@@ -236,30 +299,57 @@ def tile_gcn_pa_k_kernel(tc, x_init, adj1, W1_words, W1_scales, b1, out):
         with tc.psum_pool(name="transposed", bufs=4) as transposed, tc.psum_pool(
             name="sums", bufs=1
         ) as sums_pool:
-            for step in range(len(blocks) + LOADS_AHEAD + 1):
-                if step < len(blocks):
-                    load(step)
-                if step == len(blocks):
-                    nc.sync.dma_start(out=bias[:], in_=b1.partition_broadcast(P))
-                if 0 <= step - LOADS_AHEAD < len(blocks):
-                    sort_words(step - LOADS_AHEAD)
-                if 0 <= step - LOADS_AHEAD - 1 < len(blocks):
-                    transpose_and_quantise(step - LOADS_AHEAD - 1)
-                if 0 <= step - LOADS_AHEAD - 2 < len(blocks):
-                    multiply_block(step - LOADS_AHEAD - 2)
+            warm_sums = sums_pool.tile([P, HIDDEN], F32, name="sums3")
+
+            def keep_warm(count):
+                for i in range(count):
+                    nc.tensor.matmul(
+                        warm_sums[:], lhsT=zeros[:, 0:P], rhs=zeros[:], start=True, stop=True
+                    )
+
+            keep_warm(12)
+            banks = len(pieces) * BANKS_PER_PIECE
+            loaded = 0
+            sorted_pieces = 0
+            multiplied = 0
+            run = 0
+            runs = 0
+            for b in range(banks):
+                n = b // BANKS_PER_PIECE
+                if b % BANKS_PER_PIECE == 0:
+                    while sorted_pieces < min(len(pieces), n + 1 + SORT_AHEAD):
+                        while loaded < min(len(pieces), sorted_pieces + RAW_PIECES):
+                            load(loaded)
+                            loaded += 1
+                        sort_words(sorted_pieces)
+                        sorted_pieces += 1
+                transpose_bank(b)
+                run += 1
+                if run == (RUN_BANKS if b > 8 else 2):
+                    run = 0
+                    runs += 1
+                    if runs <= 2:
+                        keep_warm(3)
+                    while multiplied + LAG_BANKS <= b:
+                        multiply_bank(multiplied)
+                        multiplied += 1
+            late_pieces = range(first_deferred, len(pieces))
+            tail_bank = 0
 
             for i in range(PIECE_ROW_TILES):
                 nc.vector.tensor_copy(
                     out=bias_pairs[:, :, i, :], in_=bias[:].rearrange("p (h n) -> p h n", h=SIDES)
                 )
-            for j in late_blocks[:-1]:
-                multiply(j, 0, SIDE, SIDE, 0)
-            multiply_block(late_blocks[-1])
+            for n in late_pieces[0:-2:2]:
+                multiply(n, 0, PIECE_SEGMENTS, SIDE, SIDE, late_banks)
+            while multiplied < banks:
+                multiply_bank(multiplied)
+                multiplied += 1
             group_support(1, 2, 0, SIDE)
             quantise_support(1, 0, SIDE)
-            multiply(late_blocks[-1], 0, SIDE, SIDE, 0)
-            for j in late_blocks:
-                multiply(j, 1, SIDE, SIDE, 1)
+            multiply(late_pieces[-2], 0, PIECE_SEGMENTS, SIDE, SIDE, late_banks)
+            for n in late_pieces[1::2]:
+                multiply(n, 0, PIECE_SEGMENTS, SIDE, SIDE, late_banks)
             for c in range(CHUNKS):
                 multiply_adj(0, c)
             group_support(1, 2, SIDE, SIDE)

@@ -25,11 +25,11 @@ ROW_TILES = NODES // P
 PIECE_ROW_TILES = PIECE // NODES
 SIDES = 2
 SIDE = HIDDEN // SIDES
-RAW_PIECES = 12
+RAW_PIECES = 11
 SORT_AHEAD = 2
 BANKS_PER_PIECE = PIECE_SEGMENTS // BANK_SEGMENTS
-RUN_BANKS = 4
-LAG_BANKS = 4
+RUN_BANKS = 3
+LAG_SEGMENTS = 12
 
 FLOPS = 2 * NODES * FEATURES * HIDDEN + 2 * NODES * NODES * HIDDEN
 
@@ -45,9 +45,10 @@ def tile_gcn_pa_k_kernel(tc, x_init, adj1, W1_words, W1_scales, b1, out):
 
     pieces = []
     weight_after = {}
-    for g in range(4):
-        pieces.append(x_piece(0, range(PACK), [g]))
-        weight_after[len(pieces) - 1] = (g, 1)
+    for g in (0, 2):
+        for t in (0, 2):
+            pieces.append(x_piece(0, [t, t + 1], [g, g + 1]))
+        weight_after[len(pieces) - 1] = (g, 2)
     for c in range(1, CHUNKS):
         for t in range(PACK):
             pieces.append(x_piece(0, [t], chunk_passes(c)))
@@ -64,9 +65,9 @@ def tile_gcn_pa_k_kernel(tc, x_init, adj1, W1_words, W1_scales, b1, out):
 
     with tc.manual_schedule(), tc.tile_pool(name="resident", bufs=1) as resident, tc.tile_pool(
         name="raw", bufs=RAW_PIECES
-    ) as raw_pool, tc.tile_pool(name="words", bufs=5) as words_pool, tc.tile_pool(
+    ) as raw_pool, tc.tile_pool(name="words", bufs=6) as words_pool, tc.tile_pool(
         name="grouped", bufs=4
-    ) as grouped_pool, tc.tile_pool(name="operands", bufs=8) as operand_pool, tc.tile_pool(
+    ) as grouped_pool, tc.tile_pool(name="operands", bufs=11) as operand_pool, tc.tile_pool(
         name="late", bufs=CHUNKS * BLOCK_TILES
     ) as late_pool, tc.tile_pool(
         name="support", bufs=2
@@ -98,8 +99,10 @@ def tile_gcn_pa_k_kernel(tc, x_init, adj1, W1_words, W1_scales, b1, out):
         raw_of = {}
         words_of = {}
         grouped_of = {}
+        planes_of = {}
         operands_of = {}
         support_sum = {}
+        rounded_of = {}
         support_grouped = {}
 
         def load_scales(c):
@@ -145,7 +148,7 @@ def tile_gcn_pa_k_kernel(tc, x_init, adj1, W1_words, W1_scales, b1, out):
                 if count == PIECE_SEGMENTS:
                     load_scales(first // PIECE_SEGMENTS)
                 load_weight(first, count)
-            if n == 1:
+            if n == 2:
                 load_scales(0)
             if n == len(pieces) - 1:
                 nc.sync.dma_start(out=bias[:], in_=b1.partition_broadcast(P))
@@ -162,23 +165,24 @@ def tile_gcn_pa_k_kernel(tc, x_init, adj1, W1_words, W1_scales, b1, out):
                 )
             words_of[n] = words
 
-        def transpose_bank(b):
-            n, i = divmod(b, BANKS_PER_PIECE)
+        def transpose_segment(k):
+            n, i = divmod(k, PIECE_SEGMENTS)
             if i == 0:
                 grouped = grouped_pool.tile([P, PIECE_SEGMENTS, P, PACK], BF16, align_bytes=64)
                 grouped_of[n] = grouped
-            first = i * BANK_SEGMENTS
-            planes = transposed.tile([P, BANK_SEGMENTS, 2, P], F32, name="planes")
-            for k in range(BANK_SEGMENTS):
-                for u in range(2):
-                    nc.tensor.transpose(
-                        planes[:, k, u, :], words_of[n][:, first + k, u, :], identity[:]
-                    )
-            nc.scalar.copy(
-                out=grouped_of[n][:, first : first + BANK_SEGMENTS, :, :].bitcast(F32),
-                in_=planes[:].rearrange("p s u r -> p s r u"),
-            )
-            if i == BANKS_PER_PIECE - 1:
+            bank, place = divmod(i, BANK_SEGMENTS)
+            if place == 0:
+                planes = transposed.tile([P, BANK_SEGMENTS, 2, P], F32, name="planes")
+                planes_of[n, bank] = planes
+            planes = planes_of[n, bank]
+            for u in range(2):
+                nc.tensor.transpose(planes[:, place, u, :], words_of[n][:, i, u, :], identity[:])
+            if place == BANK_SEGMENTS - 1:
+                nc.scalar.copy(
+                    out=grouped_of[n][:, i + 1 - BANK_SEGMENTS : i + 1, :, :].bitcast(F32),
+                    in_=planes[:].rearrange("p s u r -> p s r u"),
+                )
+            if i == PIECE_SEGMENTS - 1:
                 quantise(n)
 
         def quantise(n):
@@ -219,6 +223,10 @@ def tile_gcn_pa_k_kernel(tc, x_init, adj1, W1_words, W1_scales, b1, out):
                 )
 
         def group_support(s, first_tile, first_column, width):
+            round_support(s, first_tile, first_column, width)
+            interleave_support(s, first_tile, first_column, width)
+
+        def round_support(s, first_tile, first_column, width):
             if first_tile == 0:
                 grouped = support_pool.tile([P, HIDDEN, PACK], BF16, align_bytes=64, name="support_grouped")
                 support_grouped[s] = grouped
@@ -228,6 +236,10 @@ def tile_gcn_pa_k_kernel(tc, x_init, adj1, W1_words, W1_scales, b1, out):
                     out=rounded[:, i, 0:width],
                     in_=support_sum[s, first_tile + i, first_column][:, 0:width],
                 )
+            rounded_of[s] = rounded
+
+        def interleave_support(s, first_tile, first_column, width):
+            rounded = rounded_of[s]
             nc.vector.tensor_copy(
                 out=support_grouped[s][
                     :, first_column : first_column + width, first_tile : first_tile + BLOCK_TILES
@@ -243,17 +255,16 @@ def tile_gcn_pa_k_kernel(tc, x_init, adj1, W1_words, W1_scales, b1, out):
                 in_=support_grouped[s][:, columns, :].rearrange("p n t -> p (n t)"),
             )
 
-        def multiply_bank(b):
-            n, i = divmod(b, BANKS_PER_PIECE)
+        def multiply_segment(k):
+            n, i = divmod(k, PIECE_SEGMENTS)
             s, segments = pieces[n]
             if s is None:
                 return
             late = n >= first_late
-            first = i * BANK_SEGMENTS
-            multiply(n, first, first + BANK_SEGMENTS, 0, SIDE if late else HIDDEN, range(PACK))
+            multiply(n, i, i + 1, 0, SIDE if late else HIDDEN, range(PACK))
             if late and n < first_deferred:
-                multiply(n, first, first + BANK_SEGMENTS, SIDE, SIDE, late_banks)
-            t, g = segments[first + BANK_SEGMENTS - 1]
+                multiply(n, i, i + 1, SIDE, SIDE, late_banks)
+            t, g = segments[i]
             if g == PASSES - 1 and t % BLOCK_TILES == BLOCK_TILES - 1 and not late:
                 group_support(s, t + 1 - BLOCK_TILES, 0, HIDDEN)
                 if t == PACK - 1:
@@ -285,7 +296,7 @@ def tile_gcn_pa_k_kernel(tc, x_init, adj1, W1_words, W1_scales, b1, out):
             y_rows[side, c] = y_sums
 
         def finish_rows(side, c):
-            rows = rows_pool.tile([P, PIECE_ROW_TILES, SIDE], F32)
+            rows = rows_pool.tile([P, PIECE_ROW_TILES, SIDE], F32, name="rows")
             nc.vector.tensor_tensor(
                 out=rows[:], in0=y_rows[side, c], in1=bias_pairs[:, side, :, :], op=mybir.AluOpType.add
             )
@@ -307,54 +318,63 @@ def tile_gcn_pa_k_kernel(tc, x_init, adj1, W1_words, W1_scales, b1, out):
                         warm_sums[:], lhsT=zeros[:, 0:P], rhs=zeros[:], start=True, stop=True
                     )
 
-            keep_warm(12)
-            banks = len(pieces) * BANKS_PER_PIECE
+            keep_warm(9)
+            total = len(pieces) * PIECE_SEGMENTS
             loaded = 0
             sorted_pieces = 0
             multiplied = 0
             run = 0
             runs = 0
-            for b in range(banks):
-                n = b // BANKS_PER_PIECE
-                if b % BANKS_PER_PIECE == 0:
-                    while sorted_pieces < min(len(pieces), n + 1 + SORT_AHEAD):
+            for k in range(total):
+                n = k // PIECE_SEGMENTS
+                if k % PIECE_SEGMENTS == 0:
+                    while sorted_pieces < min(len(pieces), n + 1 + (1 if n < 3 else 3)):
                         while loaded < min(len(pieces), sorted_pieces + RAW_PIECES):
                             load(loaded)
                             loaded += 1
                         sort_words(sorted_pieces)
                         sorted_pieces += 1
-                transpose_bank(b)
+                transpose_segment(k)
                 run += 1
-                if run == (RUN_BANKS if b > 8 else 2):
+                if run == (8 if k >= 16 else 4) or k == total - 1:
                     run = 0
                     runs += 1
-                    if runs <= 2:
-                        keep_warm(3)
-                    while multiplied + LAG_BANKS <= b:
-                        multiply_bank(multiplied)
+                    while multiplied + min(LAG_SEGMENTS, max(PIECE_SEGMENTS, k // 3)) <= k:
+                        multiply_segment(multiplied)
                         multiplied += 1
-            late_pieces = range(first_deferred, len(pieces))
+            late_pieces = list(range(first_deferred, len(pieces)))
             tail_bank = 0
 
             for i in range(PIECE_ROW_TILES):
                 nc.vector.tensor_copy(
                     out=bias_pairs[:, :, i, :], in_=bias[:].rearrange("p (h n) -> p h n", h=SIDES)
                 )
-            for n in late_pieces[0:-2:2]:
-                multiply(n, 0, PIECE_SEGMENTS, SIDE, SIDE, late_banks)
-            while multiplied < banks:
-                multiply_bank(multiplied)
+            put_off = [(n, i) for n in late_pieces[0::2] + late_pieces[1::2] for i in range(PIECE_SEGMENTS)]
+            early = PIECE_SEGMENTS * (len(late_pieces) // 2 - 1)
+
+            def multiply_put_off(first, last):
+                for n, i in put_off[first:last]:
+                    multiply(n, i, i + 1, SIDE, SIDE, late_banks)
+
+            multiply_put_off(0, early)
+            while multiplied < total:
+                multiply_segment(multiplied)
                 multiplied += 1
             group_support(1, 2, 0, SIDE)
             quantise_support(1, 0, SIDE)
-            multiply(late_pieces[-2], 0, PIECE_SEGMENTS, SIDE, SIDE, late_banks)
-            for n in late_pieces[1::2]:
-                multiply(n, 0, PIECE_SEGMENTS, SIDE, SIDE, late_banks)
-            for c in range(CHUNKS):
+            multiply_put_off(early, len(put_off) - 0)
+            for c in range(0):
                 multiply_adj(0, c)
-            group_support(1, 2, SIDE, SIDE)
+            for c in range(0):
+                finish_rows(0, c)
+            multiply_put_off(len(put_off) - 0, len(put_off))
+            for c in range(0, CHUNKS):
+                multiply_adj(0, c)
+            round_support(1, 2, SIDE, SIDE)
+            interleave_support(1, 2, SIDE, SIDE)
+            finish_rows(0, 0)
             quantise_support(1, SIDE, SIDE)
-            for c in range(CHUNKS):
+            for c in range(1, CHUNKS):
                 finish_rows(0, c)
             for c in range(CHUNKS):
                 multiply_adj(1, c)

@@ -81,14 +81,14 @@ def tile_gcn_pa_k_kernel(tc, x_init, adj1, W1_words, W1_scales, b1, out):
 
         zeros = resident.tile([P, HIDDEN], BF16)
         nc.vector.memset(zeros[:].bitcast(I32), 0)
-        w_codes = resident.tile([P, FEATURES // K_PASS, HIDDEN], U32, align_bytes=64)
-        w_scales = resident.tile([P, CHUNKS, HIDDEN], U8, align_bytes=64)
+        w_codes = resident.tile([P, FEATURES // K_PASS, HIDDEN], U32, align_bytes=256)
+        w_scales = resident.tile([P, CHUNKS, HIDDEN], U8, align_bytes=256)
         nc.vector.memset(w_scales[:].bitcast(I32), 0)
 
-        adj_codes = resident.tile([P, ROW_TILES * HALVES, P], U32, align_bytes=64)
-        adj_scales = resident.tile([P, ROW_TILES * HALVES, P], U8, align_bytes=64)
-        support_codes = resident.tile([P, HALVES, HIDDEN], U32, align_bytes=64)
-        support_scales = resident.tile([P, HALVES, HIDDEN], U8, align_bytes=64)
+        adj_codes = resident.tile([P, ROW_TILES * HALVES, P], U32, align_bytes=256)
+        adj_scales = resident.tile([P, ROW_TILES * HALVES, P], U8, align_bytes=256)
+        support_codes = resident.tile([P, HALVES, HIDDEN], U32, align_bytes=256)
+        support_scales = resident.tile([P, HALVES, HIDDEN], U8, align_bytes=256)
         bias = resident.tile([P, HIDDEN], BF16)
         bias_pairs = resident.tile([P, SIDES, PIECE_ROW_TILES, SIDE], BF16)
 
@@ -168,7 +168,7 @@ def tile_gcn_pa_k_kernel(tc, x_init, adj1, W1_words, W1_scales, b1, out):
         def transpose_segment(k):
             n, i = divmod(k, PIECE_SEGMENTS)
             if i == 0:
-                grouped = grouped_pool.tile([P, PIECE_SEGMENTS, P, PACK], BF16, align_bytes=64)
+                grouped = grouped_pool.tile([P, PIECE_SEGMENTS, P, PACK], BF16, align_bytes=256)
                 grouped_of[n] = grouped
             bank, place = divmod(i, BANK_SEGMENTS)
             if place == 0:
@@ -192,8 +192,8 @@ def tile_gcn_pa_k_kernel(tc, x_init, adj1, W1_words, W1_scales, b1, out):
                 codes, scales = adj_codes[:, chunk, :], adj_scales[:, chunk, :]
             else:
                 pool = late_pool if n >= first_late else operand_pool
-                codes_tile = pool.tile([P, PIECE_SEGMENTS, P], U32, align_bytes=64, name="codes")
-                scales_tile = pool.tile([P, PIECE_SEGMENTS, P], U8, align_bytes=64, name="scales")
+                codes_tile = pool.tile([P, PIECE_SEGMENTS, P], U32, align_bytes=256, name="codes")
+                scales_tile = pool.tile([P, PIECE_SEGMENTS, P], U8, align_bytes=256, name="scales")
                 codes, scales = codes_tile[:], scales_tile[:]
             nc.vector.quantize_mx(
                 out=codes.rearrange("p s r -> p (s r)").bitcast(FP8X4),
@@ -228,7 +228,7 @@ def tile_gcn_pa_k_kernel(tc, x_init, adj1, W1_words, W1_scales, b1, out):
 
         def round_support(s, first_tile, first_column, width):
             if first_tile == 0:
-                grouped = support_pool.tile([P, HIDDEN, PACK], BF16, align_bytes=64, name="support_grouped")
+                grouped = support_pool.tile([P, HIDDEN, PACK], BF16, align_bytes=256, name="support_grouped")
                 support_grouped[s] = grouped
             rounded = support_pool.tile([P, BLOCK_TILES, HIDDEN], BF16, name="rounded")
             for i in range(BLOCK_TILES):

@@ -46,14 +46,17 @@ def tile_gcn_pa_k_kernel(tc, x_init, adj1, W1_words, W1_scales, b1, out):
     pieces = []
     weight_after = {}
     for g in (0, 2):
-        for t in (0, 2):
-            pieces.append(x_piece(0, [t, t + 1], [g, g + 1]))
+        pieces.append(x_piece(1, [0, 1], [g, g + 1]))
         weight_after[len(pieces) - 1] = (g, 2)
+    for t in (2, 3, 0, 1):
+        pieces.append(x_piece(0, [t], chunk_passes(0)))
     for c in range(1, CHUNKS):
         for t in range(PACK):
             pieces.append(x_piece(0, [t], chunk_passes(c)))
         weight_after[len(pieces) - 1] = (c * PIECE_SEGMENTS, PIECE_SEGMENTS)
-    for c in range(CHUNKS):
+        if c in (3,):
+            pieces.append((None, (3,).index(c)))
+    for c in range(1, CHUNKS):
         for t in range(BLOCK_TILES):
             pieces.append(x_piece(1, [t], chunk_passes(c)))
         pieces.append((None, c))
@@ -67,7 +70,7 @@ def tile_gcn_pa_k_kernel(tc, x_init, adj1, W1_words, W1_scales, b1, out):
         name="raw", bufs=RAW_PIECES
     ) as raw_pool, tc.tile_pool(name="words", bufs=6) as words_pool, tc.tile_pool(
         name="grouped", bufs=4
-    ) as grouped_pool, tc.tile_pool(name="operands", bufs=11) as operand_pool, tc.tile_pool(
+    ) as grouped_pool, tc.tile_pool(name="operands", bufs=10) as operand_pool, tc.tile_pool(
         name="late", bufs=CHUNKS * BLOCK_TILES
     ) as late_pool, tc.tile_pool(
         name="support", bufs=2
@@ -90,6 +93,7 @@ def tile_gcn_pa_k_kernel(tc, x_init, adj1, W1_words, W1_scales, b1, out):
         support_codes = resident.tile([P, HALVES, HIDDEN], U32, align_bytes=256)
         support_scales = resident.tile([P, HALVES, HIDDEN], U8, align_bytes=256)
         bias = resident.tile([P, HIDDEN], BF16)
+        set_aside = resident.tile([P, BLOCK_TILES, HIDDEN], F32)
         bias_pairs = resident.tile([P, SIDES, PIECE_ROW_TILES, SIDE], BF16)
 
         x_rows = x_init.rearrange("(s p t) f -> s p t f", s=HALVES, t=PACK)
@@ -148,7 +152,7 @@ def tile_gcn_pa_k_kernel(tc, x_init, adj1, W1_words, W1_scales, b1, out):
                 if count == PIECE_SEGMENTS:
                     load_scales(first // PIECE_SEGMENTS)
                 load_weight(first, count)
-            if n == 2:
+            if n == 0:
                 load_scales(0)
             if n == len(pieces) - 1:
                 nc.sync.dma_start(out=bias[:], in_=b1.partition_broadcast(P))
@@ -209,7 +213,10 @@ def tile_gcn_pa_k_kernel(tc, x_init, adj1, W1_words, W1_scales, b1, out):
             for i in range(first, last):
                 t, g = segments[i]
                 key = (s, t, first_column)
-                if g == 0:
+                aside = s == 1 and t < BLOCK_TILES
+                starts = g == 0 or (aside and g == PIECE_SEGMENTS)
+                stops = g == PASSES - 1 or (aside and g == PIECE_SEGMENTS - 1)
+                if starts:
                     sums = sums_pool.tile([P, HIDDEN], F32, name="sums%d" % banks[t])
                     support_sum[key] = sums
                 nc.tensor.matmul_mx(
@@ -218,9 +225,11 @@ def tile_gcn_pa_k_kernel(tc, x_init, adj1, W1_words, W1_scales, b1, out):
                     lhsT_scale=scales[:, i, :],
                     rhs=w_codes[:, g, columns].bitcast(FP8X4),
                     rhs_scale=w_scales[4 * (g % PIECE_SEGMENTS) : P, g // PIECE_SEGMENTS, columns],
-                    start=(g == 0),
-                    stop=(g == PASSES - 1),
+                    start=starts,
+                    stop=stops,
                 )
+                if aside and g == PIECE_SEGMENTS - 1:
+                    nc.scalar.copy(out=set_aside[:, t, :], in_=support_sum[key][:])
 
         def group_support(s, first_tile, first_column, width):
             round_support(s, first_tile, first_column, width)
@@ -232,10 +241,13 @@ def tile_gcn_pa_k_kernel(tc, x_init, adj1, W1_words, W1_scales, b1, out):
                 support_grouped[s] = grouped
             rounded = support_pool.tile([P, BLOCK_TILES, HIDDEN], BF16, name="rounded")
             for i in range(BLOCK_TILES):
-                nc.scalar.copy(
-                    out=rounded[:, i, 0:width],
-                    in_=support_sum[s, first_tile + i, first_column][:, 0:width],
-                )
+                sums = support_sum[s, first_tile + i, first_column][:, 0:width]
+                if s == 1 and first_tile == 0:
+                    nc.vector.tensor_tensor(
+                        out=rounded[:, i, 0:width], in0=sums, in1=set_aside[:, i, :], op=mybir.AluOpType.add
+                    )
+                else:
+                    nc.scalar.copy(out=rounded[:, i, 0:width], in_=sums)
             rounded_of[s] = rounded
 
         def interleave_support(s, first_tile, first_column, width):

@@ -47,8 +47,7 @@ def tile_gcn_pa_k_kernel(tc, x_init, adj1, W1_words, W1_scales, b1, out):
     weight_after = {}
     for g in (0, 2):
         pieces.append(x_piece(1, [0, 1], [g, g + 1]))
-        weight_after[len(pieces) - 1] = (g, 2)
-    for t in (2, 3, 0, 1):
+    for t in range(PACK):
         pieces.append(x_piece(0, [t], chunk_passes(0)))
     for c in range(1, CHUNKS):
         for t in range(PACK):
@@ -147,6 +146,10 @@ def tile_gcn_pa_k_kernel(tc, x_init, adj1, W1_words, W1_scales, b1, out):
                         ],
                     )
             raw_of[n] = raw
+            if n == 1:
+                load_weight(0, 2)
+            if n == 2:
+                load_weight(2, 2)
             if n in weight_after:
                 first, count = weight_after[n]
                 if count == PIECE_SEGMENTS:
@@ -330,7 +333,7 @@ def tile_gcn_pa_k_kernel(tc, x_init, adj1, W1_words, W1_scales, b1, out):
                         warm_sums[:], lhsT=zeros[:, 0:P], rhs=zeros[:], start=True, stop=True
                     )
 
-            keep_warm(9)
+            keep_warm(6)
             total = len(pieces) * PIECE_SEGMENTS
             loaded = 0
             sorted_pieces = 0
@@ -340,7 +343,7 @@ def tile_gcn_pa_k_kernel(tc, x_init, adj1, W1_words, W1_scales, b1, out):
             for k in range(total):
                 n = k // PIECE_SEGMENTS
                 if k % PIECE_SEGMENTS == 0:
-                    while sorted_pieces < min(len(pieces), n + 1 + (1 if n < 3 else 3)):
+                    while sorted_pieces < min(len(pieces), n + 1 + (1 if n < 3 else 2 if n < 6 else 3)):
                         while loaded < min(len(pieces), sorted_pieces + RAW_PIECES):
                             load(loaded)
                             loaded += 1

import concourse.mybir as mybir
from concourse.masks import make_identity

BF16 = mybir.dt.bfloat16
F32 = mybir.dt.float32
I32 = mybir.dt.int32
U32 = mybir.dt.uint32
U8 = mybir.dt.uint8
FP8X4 = mybir.dt.float8_e4m3fn_x4

P = 128
PACK = 4
K_PASS = P * PACK
NODES, FEATURES, HIDDEN = 1024, 8192, 512

HALVES = NODES // K_PASS
PIECE_SEGMENTS = 4
PIECE = PIECE_SEGMENTS * K_PASS
CHUNKS = FEATURES // PIECE
BANK_SEGMENTS = 2
BLOCK_TILES = 2
HALF_BLOCKS = PACK // BLOCK_TILES
PASSES = FEATURES // K_PASS
ROW_TILES = NODES // P
PIECE_ROW_TILES = PIECE // NODES
SIDES = 2
SIDE = HIDDEN // SIDES
RAW_PIECES = 11
SORT_AHEAD = 2
BANKS_PER_PIECE = PIECE_SEGMENTS // BANK_SEGMENTS
RUN_BANKS = 3
LAG_SEGMENTS = 12

FLOPS = 2 * NODES * FEATURES * HIDDEN + 2 * NODES * NODES * HIDDEN


def tile_gcn_pa_k_kernel(tc, x_init, adj1, W1_words, W1_scales, b1, out):
    nc = tc.nc

    def x_piece(s, tiles, passes):
        return (s, [(t, g) for t in tiles for g in passes])

    def chunk_passes(c):
        return range(c * PIECE_SEGMENTS, (c + 1) * PIECE_SEGMENTS)

    pieces = []
    weight_after = {}
    for g in (0, 2):
        pieces.append(x_piece(1, [0, 1], [g, g + 1]))
    for t in range(PACK):
        pieces.append(x_piece(0, [t], chunk_passes(0)))
    for c in range(1, CHUNKS):
        for t in range(PACK):
            pieces.append(x_piece(0, [t], chunk_passes(c)))
        weight_after[len(pieces) - 1] = (c * PIECE_SEGMENTS, PIECE_SEGMENTS)
        if c in (3,):
            pieces.append((None, (3,).index(c)))
    for c in range(1, CHUNKS):
        for t in range(BLOCK_TILES):
            pieces.append(x_piece(1, [t], chunk_passes(c)))
        pieces.append((None, c))
    first_late = len(pieces)
    first_deferred = first_late + (CHUNKS - 2) * BLOCK_TILES
    for c in range(CHUNKS):
        for t in range(BLOCK_TILES, PACK):
            pieces.append(x_piece(1, [t], chunk_passes(c)))

    with tc.manual_schedule(), tc.tile_pool(name="resident", bufs=1) as resident, tc.tile_pool(
        name="raw", bufs=RAW_PIECES
    ) as raw_pool, tc.tile_pool(name="words", bufs=6) as words_pool, tc.tile_pool(
        name="grouped", bufs=4
    ) as grouped_pool, tc.tile_pool(name="operands", bufs=10) as operand_pool, tc.tile_pool(
        name="late", bufs=CHUNKS * BLOCK_TILES
    ) as late_pool, tc.tile_pool(
        name="support", bufs=2
    ) as support_pool, tc.tile_pool(name="rows", bufs=ROW_TILES) as rows_pool:
        identity = resident.tile([P, P], F32)
        make_identity(nc, identity[:])

        warm = resident.tile([P, 1], F32)
        nc.vector.memset(warm[:], 0.0)
        nc.scalar.activation(out=warm[:], in_=warm[:], func=mybir.ActivationFunctionType.Relu)

        zeros = resident.tile([P, HIDDEN], BF16)
        nc.vector.memset(zeros[:].bitcast(I32), 0)
        w_codes = resident.tile([P, FEATURES // K_PASS, HIDDEN], U32, align_bytes=256)
        w_scales = resident.tile([P, CHUNKS, HIDDEN], U8, align_bytes=256)
        nc.vector.memset(w_scales[:].bitcast(I32), 0)

        adj_codes = resident.tile([P, ROW_TILES * HALVES, P], U32, align_bytes=256)
        adj_scales = resident.tile([P, ROW_TILES * HALVES, P], U8, align_bytes=256)
        support_codes = resident.tile([P, HALVES, HIDDEN], U32, align_bytes=256)
        support_scales = resident.tile([P, HALVES, HIDDEN], U8, align_bytes=256)
        bias = resident.tile([P, HIDDEN], BF16)
        set_aside = resident.tile([P, BLOCK_TILES, HIDDEN], F32)
        bias_pairs = resident.tile([P, SIDES, PIECE_ROW_TILES, SIDE], BF16)

        x_rows = x_init.rearrange("(s p t) f -> s p t f", s=HALVES, t=PACK)
        adj_pieces = adj1.rearrange("(c r i) k -> c r (i k)", r=P, i=PIECE_ROW_TILES)
        out_pairs = out.rearrange("(c r i) n -> c r i n", r=P, i=PIECE_ROW_TILES)

        raw_of = {}
        words_of = {}
        grouped_of = {}
        planes_of = {}
        operands_of = {}
        support_sum = {}
        rounded_of = {}
        support_grouped = {}

        def load_scales(c):
            passes = slice(c * PIECE_SEGMENTS, (c + 1) * PIECE_SEGMENTS)
            for quadrant in range(4):
                nc.sync.dma_start(
                    out=w_scales[32 * quadrant : 32 * quadrant + 16, c, :].bitcast(I32),
                    in_=W1_scales[passes, 4 * quadrant : 4 * quadrant + 4, :].bitcast(I32),
                )

        def load_weight(first, count):
            passes = slice(first, first + count)
            nc.sync.dma_start(
                out=w_codes[:, passes, :].bitcast(I32),
                in_=W1_words[passes].rearrange("g p n t -> p g (n t)").bitcast(I32),
            )

        def load(n):
            s, segments = pieces[n]
            raw = raw_pool.tile([P, PIECE_SEGMENTS, K_PASS], BF16)
            if s is None:
                nc.sync.dma_start(
                    out=raw[:].rearrange("r s k -> r (s k)"), in_=adj_pieces[segments]
                )
            else:
                tiles = [t for t, g in segments]
                passes = [g for t, g in segments]
                first, last = min(passes), max(passes)
                count = last + 1 - first
                parts = 2 if n == 0 else 1
                step = PIECE_SEGMENTS // parts
                for i in range(0, PIECE_SEGMENTS, step):
                    part_tiles = tiles[i : i + step]
                    nc.sync.dma_start(
                        out=raw[:, i : i + step, :].rearrange("r (t g) k -> r t (g k)", g=count),
                        in_=x_rows[
                            s, :, part_tiles[0] : part_tiles[-1] + 1, first * K_PASS : (last + 1) * K_PASS
                        ],
                    )
            raw_of[n] = raw
            if n == 1:
                load_weight(0, 2)
            if n == 2:
                load_weight(2, 2)
            if n in weight_after:
                first, count = weight_after[n]
                if count == PIECE_SEGMENTS:
                    load_scales(first // PIECE_SEGMENTS)
                load_weight(first, count)
            if n == 0:
                load_scales(0)
            if n == len(pieces) - 1:
                nc.sync.dma_start(out=bias[:], in_=b1.partition_broadcast(P))

        def sort_words(n):
            words = words_pool.tile([P, PIECE_SEGMENTS, 2, P], F32)
            step = BANK_SEGMENTS if n == 0 else PIECE_SEGMENTS
            for first in range(0, PIECE_SEGMENTS, step):
                nc.vector.tensor_copy(
                    out=words[:, first : first + step, :, :],
                    in_=raw_of[n][:, first : first + step, :]
                    .bitcast(F32)
                    .rearrange("r s (p u) -> r s u p", u=2),
                )
            words_of[n] = words

        def transpose_segment(k):
            n, i = divmod(k, PIECE_SEGMENTS)
            if i == 0:
                grouped = grouped_pool.tile([P, PIECE_SEGMENTS, P, PACK], BF16, align_bytes=256)
                grouped_of[n] = grouped
            bank, place = divmod(i, BANK_SEGMENTS)
            if place == 0:
                planes = transposed.tile([P, BANK_SEGMENTS, 2, P], F32, name="planes")
                planes_of[n, bank] = planes
            planes = planes_of[n, bank]
            for u in range(2):
                nc.tensor.transpose(planes[:, place, u, :], words_of[n][:, i, u, :], identity[:])
            if place == BANK_SEGMENTS - 1:
                nc.scalar.copy(
                    out=grouped_of[n][:, i + 1 - BANK_SEGMENTS : i + 1, :, :].bitcast(F32),
                    in_=planes[:].rearrange("p s u r -> p s r u"),
                )
            if i == PIECE_SEGMENTS - 1:
                quantise(n)

        def quantise(n):
            s, segments = pieces[n]
            if s is None:
                chunk = slice(segments * PIECE_SEGMENTS, (segments + 1) * PIECE_SEGMENTS)
                codes, scales = adj_codes[:, chunk, :], adj_scales[:, chunk, :]
            else:
                pool = late_pool if n >= first_late else operand_pool
                codes_tile = pool.tile([P, PIECE_SEGMENTS, P], U32, align_bytes=256, name="codes")
                scales_tile = pool.tile([P, PIECE_SEGMENTS, P], U8, align_bytes=256, name="scales")
                codes, scales = codes_tile[:], scales_tile[:]
            nc.vector.quantize_mx(
                out=codes.rearrange("p s r -> p (s r)").bitcast(FP8X4),
                scales=scales.rearrange("p s r -> p (s r)"),
                in_=grouped_of[n][:].rearrange("p s r t -> p (s r t)"),
            )
            operands_of[n] = (codes, scales)

        def multiply(n, first, last, first_column, width, banks):
            s, segments = pieces[n]
            codes, scales = operands_of[n]
            columns = slice(first_column, first_column + width)
            for i in range(first, last):
                t, g = segments[i]
                key = (s, t, first_column)
                aside = s == 1 and t < BLOCK_TILES
                starts = g == 0 or (aside and g == PIECE_SEGMENTS)
                stops = g == PASSES - 1 or (aside and g == PIECE_SEGMENTS - 1)
                if starts:
                    sums = sums_pool.tile([P, HIDDEN], F32, name="sums%d" % banks[t])
                    support_sum[key] = sums
                nc.tensor.matmul_mx(
                    out=support_sum[key][:, 0:width],
                    lhsT=codes[:, i, :].bitcast(FP8X4),
                    lhsT_scale=scales[:, i, :],
                    rhs=w_codes[:, g, columns].bitcast(FP8X4),
                    rhs_scale=w_scales[4 * (g % PIECE_SEGMENTS) : P, g // PIECE_SEGMENTS, columns],
                    start=starts,
                    stop=stops,
                )
                if aside and g == PIECE_SEGMENTS - 1:
                    nc.scalar.copy(out=set_aside[:, t, :], in_=support_sum[key][:])

        def group_support(s, first_tile, first_column, width):
            round_support(s, first_tile, first_column, width)
            interleave_support(s, first_tile, first_column, width)

        def round_support(s, first_tile, first_column, width):
            if first_tile == 0:
                grouped = support_pool.tile([P, HIDDEN, PACK], BF16, align_bytes=256, name="support_grouped")
                support_grouped[s] = grouped
            rounded = support_pool.tile([P, BLOCK_TILES, HIDDEN], BF16, name="rounded")
            for i in range(BLOCK_TILES):
                sums = support_sum[s, first_tile + i, first_column][:, 0:width]
                if s == 1 and first_tile == 0:
                    nc.vector.tensor_tensor(
                        out=rounded[:, i, 0:width], in0=sums, in1=set_aside[:, i, :], op=mybir.AluOpType.add
                    )
                else:
                    nc.scalar.copy(out=rounded[:, i, 0:width], in_=sums)
            rounded_of[s] = rounded

        def interleave_support(s, first_tile, first_column, width):
            rounded = rounded_of[s]
            nc.vector.tensor_copy(
                out=support_grouped[s][
                    :, first_column : first_column + width, first_tile : first_tile + BLOCK_TILES
                ],
                in_=rounded[:, :, 0:width].rearrange("p t n -> p n t"),
            )

        def quantise_support(s, first_column, width):
            columns = slice(first_column, first_column + width)
            nc.vector.quantize_mx(
                out=support_codes[:, s, columns].bitcast(FP8X4),
                scales=support_scales[:, s, columns],
                in_=support_grouped[s][:, columns, :].rearrange("p n t -> p (n t)"),
            )

        def multiply_segment(k):
            n, i = divmod(k, PIECE_SEGMENTS)
            s, segments = pieces[n]
            if s is None:
                return
            late = n >= first_late
            multiply(n, i, i + 1, 0, SIDE if late else HIDDEN, range(PACK))
            if late and n < first_deferred:
                multiply(n, i, i + 1, SIDE, SIDE, late_banks)
            t, g = segments[i]
            if g == PASSES - 1 and t % BLOCK_TILES == BLOCK_TILES - 1 and not late:
                group_support(s, t + 1 - BLOCK_TILES, 0, HIDDEN)
                if t == PACK - 1:
                    quantise_support(0, 0, HIDDEN)

        y_rows = {}
        late_banks = {2: 0, 3: 1}

        def multiply_adj(side, c):
            columns = slice(side * SIDE, (side + 1) * SIDE)
            if side == 0:
                bank = transposed.tile([P, BANK_SEGMENTS, 2, P], F32, name="planes")
                y_sums = bank[:].rearrange("p i u r -> p i (u r)")
            else:
                bank = sums_pool.tile([P, HIDDEN], F32, name="sums%d" % ((2, 3, 0, 1)[c]))
                y_sums = bank[:].rearrange("p (i n) -> p i n", i=PIECE_ROW_TILES)
            for i in range(PIECE_ROW_TILES):
                for s in range(HALVES):
                    segment = (c * PIECE_ROW_TILES + i) * HALVES + s
                    nc.tensor.matmul_mx(
                        out=y_sums[:, i, :],
                        lhsT=adj_codes[:, segment, :].bitcast(FP8X4),
                        lhsT_scale=adj_scales[:, segment, :],
                        rhs=support_codes[:, s, columns].bitcast(FP8X4),
                        rhs_scale=support_scales[:, s, columns],
                        start=(s == 0),
                        stop=(s == HALVES - 1),
                    )
            y_rows[side, c] = y_sums

        def finish_rows(side, c):
            rows = rows_pool.tile([P, PIECE_ROW_TILES, SIDE], F32, name="rows")
            nc.vector.tensor_tensor(
                out=rows[:], in0=y_rows[side, c], in1=bias_pairs[:, side, :, :], op=mybir.AluOpType.add
            )
            nc.scalar.activation(
                out=rows[:], in_=rows[:], func=mybir.ActivationFunctionType.Relu
            )
            nc.sync.dma_start(
                out=out_pairs[c, :, :, side * SIDE : (side + 1) * SIDE], in_=rows[:]
            )

        with tc.psum_pool(name="transposed", bufs=4) as transposed, tc.psum_pool(
            name="sums", bufs=1
        ) as sums_pool:
            warm_sums = sums_pool.tile([P, HIDDEN], F32, name="sums3")

            def keep_warm(count):
                for i in range(count):
                    nc.tensor.matmul(
                        warm_sums[:], lhsT=zeros[:, 0:P], rhs=zeros[:], start=True, stop=True
                    )

            keep_warm(6)
            total = len(pieces) * PIECE_SEGMENTS
            loaded = 0
            sorted_pieces = 0
            multiplied = 0
            run = 0
            runs = 0
            for k in range(total):
                n = k // PIECE_SEGMENTS
                if k % PIECE_SEGMENTS == 0:
                    while sorted_pieces < min(len(pieces), n + 1 + (1 if n < 3 else 2 if n < 6 else 3)):
                        while loaded < min(len(pieces), sorted_pieces + RAW_PIECES):
                            load(loaded)
                            loaded += 1
                        sort_words(sorted_pieces)
                        sorted_pieces += 1
                transpose_segment(k)
                run += 1
                if run == (8 if k >= 16 else 4) or k == total - 1:
                    run = 0
                    runs += 1
                    while multiplied + min(LAG_SEGMENTS, max(PIECE_SEGMENTS, k // 3)) <= k:
                        multiply_segment(multiplied)
                        multiplied += 1
            late_pieces = list(range(first_deferred, len(pieces)))
            tail_bank = 0

            for i in range(PIECE_ROW_TILES):
                nc.vector.tensor_copy(
                    out=bias_pairs[:, :, i, :], in_=bias[:].rearrange("p (h n) -> p h n", h=SIDES)
                )
            put_off = [(n, i) for n in late_pieces[0::2] + late_pieces[1::2] for i in range(PIECE_SEGMENTS)]
            early = PIECE_SEGMENTS * (len(late_pieces) // 2 - 1)

            def multiply_put_off(first, last):
                for n, i in put_off[first:last]:
                    multiply(n, i, i + 1, SIDE, SIDE, late_banks)

            multiply_put_off(0, early)
            while multiplied < total:
                multiply_segment(multiplied)
                multiplied += 1
            group_support(1, 2, 0, SIDE)
            quantise_support(1, 0, SIDE)
            multiply_put_off(early, len(put_off) - 0)
            for c in range(0):
                multiply_adj(0, c)
            for c in range(0):
                finish_rows(0, c)
            multiply_put_off(len(put_off) - 0, len(put_off))
            for c in range(0, CHUNKS):
                multiply_adj(0, c)
            round_support(1, 2, SIDE, SIDE)
            interleave_support(1, 2, SIDE, SIDE)
            finish_rows(0, 0)
            quantise_support(1, SIDE, SIDE)
            for c in range(1, CHUNKS):
                finish_rows(0, c)
            for c in range(CHUNKS):
                multiply_adj(1, c)
            for c in range(CHUNKS):
                finish_rows(1, c)
